import numpy as np
import ml_dtypes


def mxq(x, axis, fmt="e4m3"):
    dtype, down = {"e4m3": (ml_dtypes.float8_e4m3fn, 7), "e5m2": (ml_dtypes.float8_e5m2, 14)}[fmt]
    v = np.moveaxis(np.asarray(x, np.float32).astype(ml_dtypes.bfloat16).astype(np.float64), axis, -1)
    blocks = v.reshape(v.shape[:-1] + (-1, 32))
    amax = np.abs(blocks).max(-1, keepdims=True)
    byte = np.maximum(np.where(amax > 0, np.frexp(amax)[1] - 1 + 127, 0) - down, 1)
    scale = np.exp2(byte - 127.0)
    codes = (blocks / scale).astype(np.float32).astype(dtype).astype(np.float64)
    return np.moveaxis((codes * scale).reshape(v.shape), -1, axis)


WIDE = False


def mx_kscale(k):
    if not WIDE:
        return np.ones(k)
    levels = np.array([10, -10, 5, -5, 0])
    if k % 512:
        return np.exp2(np.random.permutation(np.resize(levels, k // 32))).repeat(32)
    a = np.empty((k // 512, 16))
    for p in range(k // 512):
        a[p, :8] = np.random.permutation(np.resize(levels, 8))
        for g in range(8):
            far = levels[np.abs(levels - a[p, g]) >= 10]
            a[p, g + 8] = far[np.random.randint(len(far))]
    return np.exp2(a.ravel()).repeat(32)


BF16 = ml_dtypes.bfloat16


def bf(x):
    return np.asarray(x, np.float32).astype(BF16)


def f64(x):
    return np.asarray(x).astype(np.float64)


B, S, HIDDEN, H, KV, D, SEC_T, SEC_H, SEC_W, PAD = 1, 1024, 2048, 16, 2, 128, 16, 24, 24, 256
SECTIONS = (SEC_T, SEC_H, SEC_W)
VALID = S - PAD


def rotate_half(t):
    t1, t2 = np.split(t, 2, axis=-1)
    return np.concatenate((-t2, t1), axis=-1)


def reorder(t):
    chunks = []
    idx = 0
    for i in range(2 * len(SECTIONS)):
        sec = SECTIONS[i % len(SECTIONS)]
        chunks.append(t[i % len(SECTIONS), ..., idx:idx + sec])
        idx += sec
    return np.concatenate(chunks, axis=-1)


def draw0():
    sc = mx_kscale(HIDDEN)
    w = 1.0 / np.sqrt(HIDDEN)
    ang = np.random.uniform(0.0, 2.0 * np.pi, (len(SECTIONS), B, S, D))
    mask = (np.arange(S)[None, :] < VALID) * np.ones((B, 1))
    return {"x": bf(np.random.standard_normal((B, S, HIDDEN)) * sc),
            "cos": bf(np.cos(ang)), "sin": bf(np.sin(ang)), "mask": bf(mask),
            "Wq": bf(np.random.standard_normal((HIDDEN, H * D)) * w / sc[:, None]), "bq": bf(np.random.standard_normal(H * D) * 0.2),
            "Wk": bf(np.random.standard_normal((HIDDEN, KV * D)) * w / sc[:, None]), "bk": bf(np.random.standard_normal(KV * D) * 0.2),
            "Wv": bf(np.random.standard_normal((HIDDEN, KV * D)) * w / sc[:, None]), "bv": bf(np.random.standard_normal(KV * D) * 0.2)}


def core(x, cos, sin, mask, Wq, bq, Wk, bk, Wv, bv):
    xq = mxq(f64(x), 2, "e4m3")
    q = ((xq @ mxq(f64(Wq), 0, "e4m3")) + f64(bq)).reshape(B, S, H, D).transpose(0, 2, 1, 3)
    k = ((xq @ mxq(f64(Wk), 0, "e4m3")) + f64(bk)).reshape(B, S, KV, D).transpose(0, 2, 1, 3)
    v = ((xq @ mxq(f64(Wv), 0, "e4m3")) + f64(bv)).reshape(B, S, KV, D).transpose(0, 2, 1, 3)
    cos_e = reorder(f64(cos))[:, None]
    sin_e = reorder(f64(sin))[:, None]
    q = q * cos_e + rotate_half(q) * sin_e
    k = k * cos_e + rotate_half(k) * sin_e
    bm = f64(mask)[:, None, :, None]
    return q, k * bm, v * bm


def e4m3fn_bytes(y):
    return np.clip(np.asarray(y, np.float64), -448.0, 448.0).astype(np.float32).astype(ml_dtypes.float8_e4m3fn).view(np.uint8)


def e4m3fn_values(b):
    return np.asarray(b, np.uint8).view(ml_dtypes.float8_e4m3fn).astype(np.float64)


def setup_inputs():
    d = draw0()
    x0 = np.asarray(d['Wq']).astype(np.float64)
    s = (np.max(np.abs(x0), axis=(1,), keepdims=True) / 448.0).astype(np.float32)
    out = {}
    for k, v in d.items():
        if k == 'Wq':
            out['Wq_bytes'] = e4m3fn_bytes(x0 / s.astype(np.float64))
            out['Wq_scale'] = s
        else:
            out[k] = v
    return out


def reference(x, cos, sin, mask, Wq_bytes, Wq_scale, bq, Wk, bk, Wv, bv):
    return core(x, cos, sin, mask, e4m3fn_values(Wq_bytes) * Wq_scale.astype(np.float64), bq, Wk, bk, Wv, bv)

@@ -1,0 +1,338 @@
+from contextlib import ExitStack
+
+import concourse.masks as masks
+import concourse.mybir as mybir
+
+F32 = mybir.dt.float32
+BF16 = mybir.dt.bfloat16
+U8 = mybir.dt.uint8
+U32 = mybir.dt.uint32
+FP8 = mybir.dt.float8_e4m3fn
+FP8X4 = mybir.dt.float8_e4m3fn_x4
+ADD = mybir.AluOpType.add
+MULT = mybir.AluOpType.mult
+COPY = mybir.ActivationFunctionType.Copy
+IDENT = mybir.ActivationFunctionType.Identity
+
+FLOPS = 2 * 1024 * 2048 * 2560
+
+P = 128
+G = 4
+KV = 4
+ORDER = (KV, 0, 1, 2, 3)
+W_ENGS = (("p", "v"), ("p", "v"), ("p", "v"), ("p", "p"))
+SECTIONS = ((0, 0, 16), (1, 16, 24), (2, 40, 24))
+
+
+def tile_multiheadattention_pa_kernel(
+    tc, x, cos, sin, mask, Wq_bytes, Wq_scale, bq, Wk, bk, Wv, bv, out_0, out_1, out_2
+):
+    nc = tc.nc
+
+    x_v = x[0].rearrange("(j r b) (g k) -> j g r b k", j=2, r=P, b=4, g=G)
+    wq_v = Wq_bytes.rearrange("(g p t) n -> g p t n", g=G, p=P, t=4)
+    wk_v = Wk.rearrange("(g p t) n -> g p t n", g=G, p=P, t=4)
+    wv_v = Wv.rearrange("(g p t) n -> g p t n", g=G, p=P, t=4)
+    tab_v = [a[:, 0].rearrange("t (j r b) d -> j r t (b d)", j=2, r=P, b=4) for a in (cos, sin)]
+    out_v = [a[0].rearrange("h (j r b) d -> j r h (b d)", j=2, r=P, b=4) for a in (out_0, out_1, out_2)]
+
+    with ExitStack() as ctx:
+        const = ctx.enter_context(tc.tile_pool(name="const", bufs=1))
+        xr_pool = ctx.enter_context(tc.tile_pool(name="xr_pool", bufs=8))
+        wb_pool = ctx.enter_context(tc.tile_pool(name="wb_pool", bufs=8))
+        kv_pool = ctx.enter_context(tc.tile_pool(name="kv_pool", bufs=4))
+        tb_pool = ctx.enter_context(tc.tile_pool(name="tb_pool", bufs=4))
+        wc_pool = ctx.enter_context(tc.tile_pool(name="wc_pool", bufs=3))
+        xg_pool = ctx.enter_context(tc.tile_pool(name="xg_pool", bufs=2))
+        wide_pool = ctx.enter_context(tc.tile_pool(name="wide_pool", bufs=3))
+        grp_pool = ctx.enter_context(tc.tile_pool(name="grp_pool", bufs=3))
+        uw_pool = ctx.enter_context(tc.tile_pool(name="uw_pool", bufs=3))
+        o_pool = ctx.enter_context(tc.tile_pool(name="o_pool", bufs=3))
+        acc_pool = ctx.enter_context(tc.psum_pool(name="acc_pool", bufs=4))
+        tr_pool = ctx.enter_context(tc.psum_pool(name="tr_pool", bufs=4))
+
+        zero1 = const.tile([P, 1], F32, name="zero1")
+        nc.vector.memset(zero1[:], 0.0)
+        warm = const.tile([P, 1], F32, name="warm")
+        nc.scalar.activation(out=warm[:], in_=zero1[:], func=COPY)
+
+        ident_f = const.tile([P, P], F32, name="ident_f")
+        masks.make_identity(nc, ident_f[:])
+        ident_b = const.tile([P, P], BF16, name="ident_b")
+        masks.make_identity(nc, ident_b[:])
+
+        wsc = const.tile([P, 16], F32, name="wsc")
+        nc.scalar.dma_start(
+            out=wsc[:].rearrange("p (g t) -> p g t", t=4),
+            in_=Wq_scale.rearrange("(g p t) o -> p g (t o)", g=G, p=P, t=4),
+        )
+        mk_b = const.tile([P, 8], BF16, name="mk_b")
+        nc.scalar.dma_start(
+            out=mk_b[:].rearrange("p (j b) -> p j b", b=4),
+            in_=mask[0].rearrange("(j r b) -> r j b", j=2, r=P, b=4),
+        )
+        mk = const.tile([P, 8], F32, name="mk")
+        nc.vector.tensor_copy(out=mk[:], in_=mk_b[:])
+
+        brow = const.tile([P, P], BF16, name="brow")
+        nc.vector.memset(brow[:], 0.0)
+        for half in range(2):
+            for vec, row, n in ((bq, 0, 8), (bk, 8, 1), (bv, 9, 1)):
+                r0 = half * 10 + row
+                nc.scalar.dma_start(
+                    out=brow[r0 : r0 + n, :].rearrange("h (e i) -> h e i", e=2),
+                    in_=vec.rearrange("(h e f i) -> f h e i", e=2, f=2, i=64)[half],
+                )
+
+        x_codes = const.tile([P, G, 2, 512], U32, name="x_codes", align_bytes=64)
+        x_scales = const.tile([P, G, 2, 512], U8, name="x_scales", align_bytes=64)
+        tabT = const.tile([P, 4, 1024], BF16, name="tabT")
+        biasT = const.tile([P, 20], F32, name="biasT")
+
+        def copy_on(eng, out, in_):
+            if eng == "v":
+                nc.vector.tensor_copy(out=out, in_=in_)
+            elif eng == "a":
+                nc.scalar.copy(out=out, in_=in_)
+            else:
+                nc.gpsimd.tensor_scalar(out=out, in0=in_, scalar1=1.0, scalar2=0.0, op0=MULT, op1=ADD)
+
+        def load_x(j, g):
+            xr = xr_pool.tile([P, 4, 512], BF16, name="xr", tag="xr")
+            nc.sync.dma_start(out=xr[:], in_=x_v[j, g])
+            return xr
+
+        def load_w(c, g):
+            if c == KV:
+                kvraw = kv_pool.tile([P, 4, 512], BF16, name="kvraw", tag="kvraw")
+                nc.sync.dma_start(out=kvraw[:, :, 0:256], in_=wk_v[g])
+                nc.sync.dma_start(out=kvraw[:, :, 256:512], in_=wv_v[g])
+                return kvraw
+            wq_sb = wb_pool.tile([P, 4, 512], U8, name="wq_sb", tag="wq_sb")
+            nc.sync.dma_start(out=wq_sb[:], in_=wq_v[g][:, :, c * 512 : (c + 1) * 512])
+            return wq_sb
+
+        def load_tab(j):
+            raws = []
+            for a in range(2):
+                traw = tb_pool.tile([P, 3, 512], BF16, name="traw", tag="traw")
+                nc.sync.dma_start(out=traw[:], in_=tab_v[a][j])
+                raws.append(traw)
+            return raws
+
+        def prep_x(j, g, xr, eng):
+            xg = xg_pool.tile([P, 4, P, 2], F32, name="xg", tag="xg", align_bytes=64)
+            for bb in range(2):
+                xt = tr_pool.tile([P, 2, 2, P], F32, name="xt", tag="tr")
+                for b2 in range(2):
+                    words = xr[:, 2 * bb + b2, :].bitcast(F32)
+                    for u in range(2):
+                        nc.tensor.transpose(out=xt[:, b2, u, :], in_=words[:, u::2], identity=ident_f[:])
+                copy_on(eng, xg[:, 2 * bb : 2 * bb + 2, :, :], xt[:].rearrange("p b u r -> p b r u"))
+            nc.vector.quantize_mx(
+                out=x_codes[:, g, j, :].bitcast(FP8X4),
+                scales=x_scales[:, g, j, :],
+                in_=xg[:].rearrange("p b r u -> p (b r u)").bitcast(BF16),
+            )
+
+        def widen(g, wq_sb):
+            wide = wide_pool.tile([P, 4, 512], BF16, name="wide", tag="wide")
+            for t in range(4):
+                nc.scalar.activation(
+                    out=wide[:, t, :],
+                    in_=wq_sb[:, t, :].bitcast(FP8),
+                    func=COPY,
+                    scale=wsc[:, 4 * g + t : 4 * g + t + 1],
+                )
+            return wide
+
+        def group_and_quantize(g, wide, codes, scales, engs):
+            grp = grp_pool.tile([P, 2048], BF16, name="grp", tag="grp", align_bytes=64)
+            dst = grp[:].rearrange("p (f h i t) -> p f h i t", f=2, h=4, i=64)
+            src = wide[:].rearrange("p t (h f i) -> p f h i t", h=4, f=2)
+            for half in range(2):
+                copy_on(engs[half], dst[:, half], src[:, half])
+            nc.vector.quantize_mx(out=codes[:, g, :].bitcast(FP8X4), scales=scales[:, g, :], in_=grp[:])
+
+        def new_w_tiles():
+            codes = wc_pool.tile([P, G, 512], U32, name="w_codes", tag="w_codes", align_bytes=64)
+            scales = wc_pool.tile([P, G, 512], U8, name="w_scales", tag="w_scales", align_bytes=64)
+            return codes, scales
+
+        def build_tables(j, raws, eng):
+            for a in range(2):
+                asm = tb_pool.tile([P, 4, 256], BF16, name="asm", tag="asm")
+                dst = asm[:].rearrange("p b (f d i) -> p b f d i", f=2, d=2)
+                src = raws[a][:].rearrange("p t (b f i) -> p t b f i", b=4, f=2)
+                for tb, c0, n in SECTIONS:
+                    for dup in range(2):
+                        copy_on(eng, dst[:, :, :, dup, c0 : c0 + n], src[:, tb, :, :, c0 : c0 + n])
+                for half in range(2):
+                    pt = tr_pool.tile([P, 4, P], BF16, name="pt", tag="tr")
+                    for b in range(4):
+                        nc.tensor.transpose(
+                            out=pt[:, b, :], in_=asm[:, b, half * P : (half + 1) * P], identity=ident_b[:]
+                        )
+                    nc.scalar.activation(
+                        out=tabT[:, 2 * a + half, j * 512 : (j + 1) * 512],
+                        in_=pt[:].rearrange("p b r -> p (b r)"),
+                        func=COPY,
+                        scale=(-1.0 if (a == 1 and half == 0) else 1.0),
+                    )
+
+        def new_acc():
+            acc_a = acc_pool.tile([P, 512], F32, name="acc_a", tag="acc")
+            acc_b = acc_pool.tile([P, 512], F32, name="acc_b", tag="acc")
+            return (acc_a, acc_b)
+
+        def mx(wt, q, j, half, g, acc):
+            cols = slice((half * 2 + q) * P, (half * 2 + q + 1) * P)
+            nc.tensor.matmul_mx(
+                out=acc[:],
+                lhsT=wt[0][:, g, cols].bitcast(FP8X4),
+                lhsT_scale=wt[1][:, g, cols],
+                rhs=x_codes[:, g, j, :].bitcast(FP8X4),
+                rhs_scale=x_scales[:, g, j, :],
+                start=(g == 0),
+                stop=(g == G - 1),
+            )
+
+        def rope(c, q, j, accs):
+            hp = 2 * c + q
+            b_lo = biasT[:, hp : hp + 1]
+            b_hi = biasT[:, 10 + hp : 11 + hp]
+            cols = slice(j * 512, (j + 1) * 512)
+            u_lo = uw_pool.tile([P, 512], F32, name="u_lo", tag="u_lo")
+            u_hi = uw_pool.tile([P, 512], F32, name="u_hi", tag="u_hi")
+            if hp == 9:
+                nc.vector.tensor_scalar(out=u_lo[:], in0=accs[0][:], scalar1=b_lo, scalar2=None, op0=ADD)
+                nc.scalar.activation(out=u_hi[:], in_=accs[1][:], func=IDENT, bias=b_hi)
+                return ((u_lo, None), (u_hi, None))
+            w_lo = uw_pool.tile([P, 512], F32, name="w_lo", tag="w_lo")
+            w_hi = uw_pool.tile([P, 512], F32, name="w_hi", tag="w_hi")
+            for out, acc, bias, k in (
+                (u_lo, accs[0], b_lo, 0),
+                (w_hi, accs[0], b_lo, 3),
+                (w_lo, accs[1], b_hi, 2),
+                (u_hi, accs[1], b_hi, 1),
+            ):
+                nc.vector.scalar_tensor_tensor(
+                    out=out[:], in0=acc[:], scalar=bias, in1=tabT[:, k, cols], op0=ADD, op1=MULT
+                )
+            pairs = []
+            for half, (u, w) in enumerate(((u_lo, w_lo), (u_hi, w_hi))):
+                if half == 0 or (q == 1 and j == 1):
+                    pairs.append((u, w))
+                else:
+                    nc.vector.tensor_tensor(out=u[:], in0=u[:], in1=w[:], op=ADD)
+                    pairs.append((u, None))
+            return tuple(pairs)
+
+        def turn_back(dst, pair, b):
+            u, w = pair
+            bs = slice(b * P, (b + 1) * P)
+            if w is None:
+                nc.tensor.transpose(out=dst, in_=u[:, bs], identity=ident_f[:])
+            else:
+                nc.tensor.matmul(out=dst, lhsT=u[:, bs], rhs=ident_f[:], is_transpose=True, start=True, stop=False)
+                nc.tensor.matmul(out=dst, lhsT=w[:, bs], rhs=ident_f[:], is_transpose=True, start=False, stop=True)
+
+        def back(c, q, j, pairs):
+            o = o_pool.tile([P, 2, 4, 2, 64], F32, name="o", tag="o")
+            for half in range(2):
+                ob = tr_pool.tile([P, 4, P], F32, name="ob", tag="tr")
+                for b in range(4):
+                    turn_back(ob[:, b, :], pairs[half], b)
+                nc.scalar.copy(
+                    out=o[:, :, :, half, :].rearrange("p e b i -> p b e i"),
+                    in_=ob[:].rearrange("p b (e i) -> p b e i", e=2),
+                )
+            nc.sync.dma_start(
+                out=out_v[0][j][:, 4 * c + 2 * q : 4 * c + 2 * q + 2, :],
+                in_=o[:].rearrange("p e b f i -> p e (b f i)"),
+            )
+
+        def back_kv(j, pairs_kv):
+            okv = o_pool.tile([P, 2, 2, 4, 2, 64], F32, name="okv", tag="okv", bufs=2)
+            for b in range(4):
+                ob = tr_pool.tile([P, 2, 2, P], F32, name="obkv", tag="tr")
+                for kv in range(2):
+                    for half in range(2):
+                        turn_back(ob[:, half, kv, :], pairs_kv[kv][half], b)
+                nc.scalar.activation(
+                    out=okv[:, :, :, b, :, :].rearrange("p k e f i -> p (k e) f i"),
+                    in_=ob[:].rearrange("p f k (e i) -> p (k e) f i", e=2),
+                    func=COPY,
+                    scale=mk[:, 4 * j + b : 4 * j + b + 1],
+                )
+            for kv in range(2):
+                nc.sync.dma_start(out=out_v[1 + kv][j], in_=okv[:, kv].rearrange("p e b f i -> p e (b f i)"))
+
+        first, second = ORDER[0], ORDER[1]
+        xr = {}
+        wraw = {}
+        for g in range(G):
+            xr[(0, g)] = load_x(0, g)
+            wraw[(first, g)] = load_w(first, g)
+        traw0 = load_tab(0)
+        for g in range(G):
+            wraw[(second, g)] = load_w(second, g)
+        for g in range(G):
+            xr[(1, g)] = load_x(1, g)
+        traw1 = load_tab(1)
+        for g in range(G):
+            wraw[(ORDER[2], g)] = load_w(ORDER[2], g)
+
+        wts = {}
+
+        def w_slice(c, g, engs):
+            if g == 0:
+                wts[c] = new_w_tiles()
+            raw = wraw[(c, g)]
+            wide = raw if c == KV else widen(g, raw)
+            group_and_quantize(g, wide, wts[c][0], wts[c][1], engs)
+
+        def head(j, units, eng):
+            accs = [new_acc() for unit in units]
+            for g in range(G):
+                prep_x(j, g, xr[(j, g)], eng)
+                if j == 0:
+                    w_slice(first, g, ("a", "p"))
+                for n, (c, q) in enumerate(units):
+                    for half in range(2):
+                        mx(wts[c], q, j, half, g, accs[n][half])
+            return accs
+
+        units = ((first, 0), (first, 1))
+        accs0 = head(0, units, "a")
+        pb = tr_pool.tile([P, P], BF16, name="pb", tag="tr")
+        nc.tensor.transpose(out=pb[:], in_=brow[:], identity=ident_b[:])
+        nc.vector.tensor_copy(out=biasT[:], in_=pb[:, 0:20])
+        build_tables(0, traw0, "p")
+        for g in range(G):
+            w_slice(second, g, W_ENGS[g])
+        pairs0 = [rope(c, q, 0, accs0[n]) for n, (c, q) in enumerate(units)]
+        accs1 = head(1, units, "a")
+        back_kv(0, pairs0)
+        build_tables(1, traw1, "p")
+        pairs1 = [rope(c, q, 1, accs1[n]) for n, (c, q) in enumerate(units)]
+        pending = []
+
+        for ci in range(1, len(ORDER)):
+            c = ORDER[ci]
+            for n, (q, j) in enumerate(((0, 0), (0, 1), (1, 0), (1, 1))):
+                accs = new_acc()
+                for half in range(2):
+                    for g in range(G):
+                        mx(wts[c], q, j, half, g, accs[half])
+                if ci == 1 and n == 0:
+                    back_kv(1, pairs1)
+                for item in pending:
+                    back(item[0], item[1], item[2], item[3])
+                pending = [(c, q, j, rope(c, q, j, accs))]
+                if ci + 1 < len(ORDER):
+                    w_slice(ORDER[ci + 1], n, W_ENGS[n])
+                if ci + 2 < len(ORDER):
+                    wraw[(ORDER[ci + 2], n)] = load_w(ORDER[ci + 2], n)
+        for item in pending:
+            back(item[0], item[1], item[2], item[3])

@@ -19,8 +19,6 @@ FLOPS = 2 * 1024 * 2048 * 2560
 P = 128
 G = 4
 KV = 4
-ORDER = (KV, 0, 1, 2, 3)
-W_ENGS = (("p", "v"), ("p", "v"), ("p", "v"), ("p", "p"))
 SECTIONS = ((0, 0, 16), (1, 16, 24), (2, 40, 24))
 
 
@@ -38,8 +36,8 @@ def tile_multiheadattention_pa_kernel(
 
     with ExitStack() as ctx:
         const = ctx.enter_context(tc.tile_pool(name="const", bufs=1))
-        xr_pool = ctx.enter_context(tc.tile_pool(name="xr_pool", bufs=8))
-        wb_pool = ctx.enter_context(tc.tile_pool(name="wb_pool", bufs=8))
+        xr_pool = ctx.enter_context(tc.tile_pool(name="xr_pool", bufs=6))
+        wb_pool = ctx.enter_context(tc.tile_pool(name="wb_pool", bufs=16))
         kv_pool = ctx.enter_context(tc.tile_pool(name="kv_pool", bufs=4))
         tb_pool = ctx.enter_context(tc.tile_pool(name="tb_pool", bufs=4))
         wc_pool = ctx.enter_context(tc.tile_pool(name="wc_pool", bufs=3))
@@ -50,40 +48,22 @@ def tile_multiheadattention_pa_kernel(
         o_pool = ctx.enter_context(tc.tile_pool(name="o_pool", bufs=3))
         acc_pool = ctx.enter_context(tc.psum_pool(name="acc_pool", bufs=4))
         tr_pool = ctx.enter_context(tc.psum_pool(name="tr_pool", bufs=4))
+        ctx.enter_context(tc.manual_schedule())
 
         zero1 = const.tile([P, 1], F32, name="zero1")
         nc.vector.memset(zero1[:], 0.0)
         warm = const.tile([P, 1], F32, name="warm")
         nc.scalar.activation(out=warm[:], in_=zero1[:], func=COPY)
-
+        brow = const.tile([P, P], BF16, name="brow")
+        nc.vector.memset(brow[:], 0.0)
         ident_f = const.tile([P, P], F32, name="ident_f")
         masks.make_identity(nc, ident_f[:])
         ident_b = const.tile([P, P], BF16, name="ident_b")
         masks.make_identity(nc, ident_b[:])
 
         wsc = const.tile([P, 16], F32, name="wsc")
-        nc.scalar.dma_start(
-            out=wsc[:].rearrange("p (g t) -> p g t", t=4),
-            in_=Wq_scale.rearrange("(g p t) o -> p g (t o)", g=G, p=P, t=4),
-        )
         mk_b = const.tile([P, 8], BF16, name="mk_b")
-        nc.scalar.dma_start(
-            out=mk_b[:].rearrange("p (j b) -> p j b", b=4),
-            in_=mask[0].rearrange("(j r b) -> r j b", j=2, r=P, b=4),
-        )
         mk = const.tile([P, 8], F32, name="mk")
-        nc.vector.tensor_copy(out=mk[:], in_=mk_b[:])
-
-        brow = const.tile([P, P], BF16, name="brow")
-        nc.vector.memset(brow[:], 0.0)
-        for half in range(2):
-            for vec, row, n in ((bq, 0, 8), (bk, 8, 1), (bv, 9, 1)):
-                r0 = half * 10 + row
-                nc.scalar.dma_start(
-                    out=brow[r0 : r0 + n, :].rearrange("h (e i) -> h e i", e=2),
-                    in_=vec.rearrange("(h e f i) -> f h e i", e=2, f=2, i=64)[half],
-                )
-
         x_codes = const.tile([P, G, 2, 512], U32, name="x_codes", align_bytes=64)
         x_scales = const.tile([P, G, 2, 512], U8, name="x_scales", align_bytes=64)
         tabT = const.tile([P, 4, 1024], BF16, name="tabT")
@@ -97,242 +77,375 @@ def tile_multiheadattention_pa_kernel(
             else:
                 nc.gpsimd.tensor_scalar(out=out, in0=in_, scalar1=1.0, scalar2=0.0, op0=MULT, op1=ADD)
 
+        xr = {}
+        wraw = {}
+        traw = {}
+
         def load_x(j, g):
-            xr = xr_pool.tile([P, 4, 512], BF16, name="xr", tag="xr")
-            nc.sync.dma_start(out=xr[:], in_=x_v[j, g])
-            return xr
+            xr[(j, g)] = xr_pool.tile([P, 4, 512], BF16, name="xr", tag="xr")
+            nc.sync.dma_start(out=xr[(j, g)][:], in_=x_v[j, g])
 
         def load_w(c, g):
             if c == KV:
                 kvraw = kv_pool.tile([P, 4, 512], BF16, name="kvraw", tag="kvraw")
                 nc.sync.dma_start(out=kvraw[:, :, 0:256], in_=wk_v[g])
                 nc.sync.dma_start(out=kvraw[:, :, 256:512], in_=wv_v[g])
-                return kvraw
-            wq_sb = wb_pool.tile([P, 4, 512], U8, name="wq_sb", tag="wq_sb")
-            nc.sync.dma_start(out=wq_sb[:], in_=wq_v[g][:, :, c * 512 : (c + 1) * 512])
-            return wq_sb
+                wraw[(c, g)] = kvraw
+            else:
+                wq_sb = wb_pool.tile([P, 4, 512], U8, name="wq_sb", tag="wq_sb")
+                nc.sync.dma_start(out=wq_sb[:], in_=wq_v[g][:, :, c * 512 : (c + 1) * 512])
+                wraw[(c, g)] = wq_sb
 
         def load_tab(j):
-            raws = []
             for a in range(2):
-                traw = tb_pool.tile([P, 3, 512], BF16, name="traw", tag="traw")
-                nc.sync.dma_start(out=traw[:], in_=tab_v[a][j])
-                raws.append(traw)
-            return raws
+                traw[(j, a)] = tb_pool.tile([P, 3, 512], BF16, name="traw", tag="traw")
+                nc.sync.dma_start(out=traw[(j, a)][:], in_=tab_v[a][j])
 
-        def prep_x(j, g, xr, eng):
-            xg = xg_pool.tile([P, 4, P, 2], F32, name="xg", tag="xg", align_bytes=64)
+        def load_wsc():
+            nc.sync.dma_start(
+                out=wsc[:].rearrange("p (g t) -> p g t", t=4),
+                in_=Wq_scale.rearrange("(g p t) o -> p g (t o)", g=G, p=P, t=4),
+            )
+
+        def load_mask():
+            nc.sync.dma_start(
+                out=mk_b[:].rearrange("p (j b) -> p j b", b=4),
+                in_=mask[0].rearrange("(j r b) -> r j b", j=2, r=P, b=4),
+            )
+
+        def load_bias(half):
+            for vec, row, n in ((bq, 0, 8), (bk, 8, 1), (bv, 9, 1)):
+                r0 = half * 10 + row
+                nc.sync.dma_start(
+                    out=brow[r0 : r0 + n, :].rearrange("h (e i) -> h e i", e=2),
+                    in_=vec.rearrange("(h e f i) -> f h e i", e=2, f=2, i=64)[half],
+                )
+
+        xt = {}
+        xg = {}
+
+        def x_turn(j, g):
             for bb in range(2):
-                xt = tr_pool.tile([P, 2, 2, P], F32, name="xt", tag="tr")
+                t = tr_pool.tile([P, 2, 2, P], F32, name="xt", tag="tr")
+                xt[(j, g, bb)] = t
                 for b2 in range(2):
-                    words = xr[:, 2 * bb + b2, :].bitcast(F32)
+                    words = xr[(j, g)][:, 2 * bb + b2, :].bitcast(F32)
                     for u in range(2):
-                        nc.tensor.transpose(out=xt[:, b2, u, :], in_=words[:, u::2], identity=ident_f[:])
-                copy_on(eng, xg[:, 2 * bb : 2 * bb + 2, :, :], xt[:].rearrange("p b u r -> p b r u"))
+                        nc.tensor.transpose(out=t[:, b2, u, :], in_=words[:, u::2], identity=ident_f[:])
+
+        def x_out(j, g, eng):
+            xg[(j, g)] = xg_pool.tile([P, 4, P, 2], F32, name="xg", tag="xg", align_bytes=64)
+            for bb in range(2):
+                copy_on(eng[bb], xg[(j, g)][:, 2 * bb : 2 * bb + 2, :, :], xt[(j, g, bb)][:].rearrange("p b u r -> p b r u"))
+
+        def x_quant(j, g):
             nc.vector.quantize_mx(
                 out=x_codes[:, g, j, :].bitcast(FP8X4),
                 scales=x_scales[:, g, j, :],
-                in_=xg[:].rearrange("p b r u -> p (b r u)").bitcast(BF16),
+                in_=xg[(j, g)][:].rearrange("p b r u -> p (b r u)").bitcast(BF16),
             )
 
-        def widen(g, wq_sb):
-            wide = wide_pool.tile([P, 4, 512], BF16, name="wide", tag="wide")
+        wide = {}
+        grp = {}
+        wts = {}
+
+        def w_widen(c, g):
+            wide[(c, g)] = wide_pool.tile([P, 4, 512], BF16, name="wide", tag="wide")
             for t in range(4):
                 nc.scalar.activation(
-                    out=wide[:, t, :],
-                    in_=wq_sb[:, t, :].bitcast(FP8),
+                    out=wide[(c, g)][:, t, :],
+                    in_=wraw[(c, g)][:, t, :].bitcast(FP8),
                     func=COPY,
                     scale=wsc[:, 4 * g + t : 4 * g + t + 1],
                 )
-            return wide
 
-        def group_and_quantize(g, wide, codes, scales, engs):
-            grp = grp_pool.tile([P, 2048], BF16, name="grp", tag="grp", align_bytes=64)
-            dst = grp[:].rearrange("p (f h i t) -> p f h i t", f=2, h=4, i=64)
-            src = wide[:].rearrange("p t (h f i) -> p f h i t", h=4, f=2)
+        def w_group(c, g, engs):
+            grp[(c, g)] = grp_pool.tile([P, 2048], BF16, name="grp", tag="grp", align_bytes=64)
+            source = wraw[(c, g)] if c == KV else wide[(c, g)]
+            dst = grp[(c, g)][:].rearrange("p (f h i t) -> p f h i t", f=2, h=4, i=64)
+            src = source[:].rearrange("p t (h f i) -> p f h i t", h=4, f=2)
             for half in range(2):
                 copy_on(engs[half], dst[:, half], src[:, half])
-            nc.vector.quantize_mx(out=codes[:, g, :].bitcast(FP8X4), scales=scales[:, g, :], in_=grp[:])
 
-        def new_w_tiles():
-            codes = wc_pool.tile([P, G, 512], U32, name="w_codes", tag="w_codes", align_bytes=64)
-            scales = wc_pool.tile([P, G, 512], U8, name="w_scales", tag="w_scales", align_bytes=64)
-            return codes, scales
+        def w_quant(c, g):
+            if g == 0:
+                codes = wc_pool.tile([P, G, 512], U32, name="w_codes", tag="w_codes", align_bytes=64)
+                scales = wc_pool.tile([P, G, 512], U8, name="w_scales", tag="w_scales", align_bytes=64)
+                wts[c] = (codes, scales)
+            nc.vector.quantize_mx(
+                out=wts[c][0][:, g, :].bitcast(FP8X4), scales=wts[c][1][:, g, :], in_=grp[(c, g)][:]
+            )
 
-        def build_tables(j, raws, eng):
-            for a in range(2):
-                asm = tb_pool.tile([P, 4, 256], BF16, name="asm", tag="asm")
-                dst = asm[:].rearrange("p b (f d i) -> p b f d i", f=2, d=2)
-                src = raws[a][:].rearrange("p t (b f i) -> p t b f i", b=4, f=2)
-                for tb, c0, n in SECTIONS:
-                    for dup in range(2):
-                        copy_on(eng, dst[:, :, :, dup, c0 : c0 + n], src[:, tb, :, :, c0 : c0 + n])
-                for half in range(2):
-                    pt = tr_pool.tile([P, 4, P], BF16, name="pt", tag="tr")
-                    for b in range(4):
-                        nc.tensor.transpose(
-                            out=pt[:, b, :], in_=asm[:, b, half * P : (half + 1) * P], identity=ident_b[:]
-                        )
-                    nc.scalar.activation(
-                        out=tabT[:, 2 * a + half, j * 512 : (j + 1) * 512],
-                        in_=pt[:].rearrange("p b r -> p (b r)"),
-                        func=COPY,
-                        scale=(-1.0 if (a == 1 and half == 0) else 1.0),
+        asm = {}
+
+        def tab_gather(j, a, eng):
+            asm[(j, a)] = tb_pool.tile([P, 4, 256], BF16, name="asm", tag="asm")
+            dst = asm[(j, a)][:].rearrange("p b (f d i) -> p b f d i", f=2, d=2)
+            src = traw[(j, a)][:].rearrange("p t (b f i) -> p t b f i", b=4, f=2)
+            for tb, c0, n in SECTIONS:
+                for dup in range(2):
+                    copy_on(eng, dst[:, :, :, dup, c0 : c0 + n], src[:, tb, :, :, c0 : c0 + n])
+
+        def tab_turn(j, a, eng):
+            for half in range(2):
+                pt = tr_pool.tile([P, 4, P], BF16, name="pt", tag="tr")
+                for b in range(4):
+                    nc.tensor.transpose(
+                        out=pt[:, b, :], in_=asm[(j, a)][:, b, half * P : (half + 1) * P], identity=ident_b[:]
+                    )
+                sign = -1.0 if (a == 1 and half == 0) else 1.0
+                dst = tabT[:, 2 * a + half, j * 512 : (j + 1) * 512]
+                if eng == "a":
+                    nc.scalar.activation(out=dst, in_=pt[:].rearrange("p b r -> p (b r)"), func=COPY, scale=sign)
+                else:
+                    nc.vector.tensor_scalar(
+                        out=dst, in0=pt[:].rearrange("p b r -> p (b r)"), scalar1=sign, scalar2=None, op0=MULT
                     )
 
-        def new_acc():
-            acc_a = acc_pool.tile([P, 512], F32, name="acc_a", tag="acc")
-            acc_b = acc_pool.tile([P, 512], F32, name="acc_b", tag="acc")
-            return (acc_a, acc_b)
+        def bias_turn():
+            pb = tr_pool.tile([P, P], BF16, name="pb", tag="tr")
+            nc.tensor.transpose(out=pb[:], in_=brow[:], identity=ident_b[:])
+            nc.vector.tensor_copy(out=biasT[:], in_=pb[:, 0:20])
+            nc.vector.tensor_copy(out=mk[:], in_=mk_b[:])
 
-        def mx(wt, q, j, half, g, acc):
+        accs = {}
+        uw = {}
+        summed = set()
+
+        def mx(unit, half, g):
+            c, q, j = unit
+            if g == 0:
+                accs[(unit, half)] = acc_pool.tile([P, 512], F32, name="acc", tag="acc")
             cols = slice((half * 2 + q) * P, (half * 2 + q + 1) * P)
             nc.tensor.matmul_mx(
-                out=acc[:],
-                lhsT=wt[0][:, g, cols].bitcast(FP8X4),
-                lhsT_scale=wt[1][:, g, cols],
+                out=accs[(unit, half)][:],
+                lhsT=wts[c][0][:, g, cols].bitcast(FP8X4),
+                lhsT_scale=wts[c][1][:, g, cols],
                 rhs=x_codes[:, g, j, :].bitcast(FP8X4),
                 rhs_scale=x_scales[:, g, j, :],
                 start=(g == 0),
                 stop=(g == G - 1),
             )
 
-        def rope(c, q, j, accs):
+        def rope(unit, half):
+            c, q, j = unit
             hp = 2 * c + q
-            b_lo = biasT[:, hp : hp + 1]
-            b_hi = biasT[:, 10 + hp : 11 + hp]
-            cols = slice(j * 512, (j + 1) * 512)
-            u_lo = uw_pool.tile([P, 512], F32, name="u_lo", tag="u_lo")
-            u_hi = uw_pool.tile([P, 512], F32, name="u_hi", tag="u_hi")
+            bias = biasT[:, 10 * half + hp : 10 * half + hp + 1]
+            acc = accs[(unit, half)]
             if hp == 9:
-                nc.vector.tensor_scalar(out=u_lo[:], in0=accs[0][:], scalar1=b_lo, scalar2=None, op0=ADD)
-                nc.scalar.activation(out=u_hi[:], in_=accs[1][:], func=IDENT, bias=b_hi)
-                return ((u_lo, None), (u_hi, None))
-            w_lo = uw_pool.tile([P, 512], F32, name="w_lo", tag="w_lo")
-            w_hi = uw_pool.tile([P, 512], F32, name="w_hi", tag="w_hi")
-            for out, acc, bias, k in (
-                (u_lo, accs[0], b_lo, 0),
-                (w_hi, accs[0], b_lo, 3),
-                (w_lo, accs[1], b_hi, 2),
-                (u_hi, accs[1], b_hi, 1),
-            ):
+                name = ("u_lo", "u_hi")[half]
+                uw[(unit, name)] = uw_pool.tile([P, 512], F32, name=name, tag=name)
+                nc.vector.tensor_scalar(out=uw[(unit, name)][:], in0=acc[:], scalar1=bias, scalar2=None, op0=ADD)
+                return
+            for name, k in ((("u_lo", 0), ("w_hi", 3)), (("w_lo", 2), ("u_hi", 1)))[half]:
+                uw[(unit, name)] = uw_pool.tile([P, 512], F32, name=name, tag=name)
                 nc.vector.scalar_tensor_tensor(
-                    out=out[:], in0=acc[:], scalar=bias, in1=tabT[:, k, cols], op0=ADD, op1=MULT
+                    out=uw[(unit, name)][:],
+                    in0=acc[:],
+                    scalar=bias,
+                    in1=tabT[:, k, j * 512 : (j + 1) * 512],
+                    op0=ADD,
+                    op1=MULT,
                 )
-            pairs = []
-            for half, (u, w) in enumerate(((u_lo, w_lo), (u_hi, w_hi))):
-                if half == 0 or (q == 1 and j == 1):
-                    pairs.append((u, w))
-                else:
-                    nc.vector.tensor_tensor(out=u[:], in0=u[:], in1=w[:], op=ADD)
-                    pairs.append((u, None))
-            return tuple(pairs)
 
-        def turn_back(dst, pair, b):
-            u, w = pair
+        def add_on(eng, unit, half):
+            u = uw[(unit, ("u_lo", "u_hi")[half])]
+            w = uw[(unit, ("w_lo", "w_hi")[half])]
+            summed.add((unit, half))
+            if eng == "v":
+                nc.vector.tensor_tensor(out=u[:], in0=u[:], in1=w[:], op=ADD)
+            else:
+                nc.gpsimd.tensor_tensor(out=u[:], in0=u[:], in1=w[:], op=ADD)
+
+        def turn_back(dst, unit, half, b):
+            u = uw[(unit, ("u_lo", "u_hi")[half])]
+            w = uw.get((unit, ("w_lo", "w_hi")[half]))
             bs = slice(b * P, (b + 1) * P)
-            if w is None:
+            if w is None or (unit, half) in summed:
                 nc.tensor.transpose(out=dst, in_=u[:, bs], identity=ident_f[:])
             else:
                 nc.tensor.matmul(out=dst, lhsT=u[:, bs], rhs=ident_f[:], is_transpose=True, start=True, stop=False)
                 nc.tensor.matmul(out=dst, lhsT=w[:, bs], rhs=ident_f[:], is_transpose=True, start=False, stop=True)
 
-        def back(c, q, j, pairs):
-            o = o_pool.tile([P, 2, 4, 2, 64], F32, name="o", tag="o")
-            for half in range(2):
-                ob = tr_pool.tile([P, 4, P], F32, name="ob", tag="tr")
-                for b in range(4):
-                    turn_back(ob[:, b, :], pairs[half], b)
-                nc.scalar.copy(
-                    out=o[:, :, :, half, :].rearrange("p e b i -> p b e i"),
-                    in_=ob[:].rearrange("p b (e i) -> p b e i", e=2),
-                )
-            nc.sync.dma_start(
-                out=out_v[0][j][:, 4 * c + 2 * q : 4 * c + 2 * q + 2, :],
-                in_=o[:].rearrange("p e b f i -> p e (b f i)"),
+        ob = {}
+        o_sb = {}
+
+        def back_turn(unit, half):
+            ob[(unit, half)] = tr_pool.tile([P, 4, P], F32, name="ob", tag="tr")
+            for b in range(4):
+                turn_back(ob[(unit, half)][:, b, :], unit, half, b)
+
+        def back_out(unit, half):
+            if half == 0:
+                o_sb[unit] = o_pool.tile([P, 2, 4, 2, 64], F32, name="o", tag="o")
+            nc.scalar.copy(
+                out=o_sb[unit][:, :, :, half, :].rearrange("p e b i -> p b e i"),
+                in_=ob[(unit, half)][:].rearrange("p b (e i) -> p b e i", e=2),
             )
 
-        def back_kv(j, pairs_kv):
-            okv = o_pool.tile([P, 2, 2, 4, 2, 64], F32, name="okv", tag="okv", bufs=2)
-            for b in range(4):
-                ob = tr_pool.tile([P, 2, 2, P], F32, name="obkv", tag="tr")
-                for kv in range(2):
-                    for half in range(2):
-                        turn_back(ob[:, half, kv, :], pairs_kv[kv][half], b)
-                nc.scalar.activation(
-                    out=okv[:, :, :, b, :, :].rearrange("p k e f i -> p (k e) f i"),
-                    in_=ob[:].rearrange("p f k (e i) -> p (k e) f i", e=2),
-                    func=COPY,
-                    scale=mk[:, 4 * j + b : 4 * j + b + 1],
-                )
-            for kv in range(2):
-                nc.sync.dma_start(out=out_v[1 + kv][j], in_=okv[:, kv].rearrange("p e b f i -> p e (b f i)"))
+        def back_store(unit):
+            c, q, j = unit
+            nc.sync.dma_start(
+                out=out_v[0][j][:, 4 * c + 2 * q : 4 * c + 2 * q + 2, :],
+                in_=o_sb[unit][:].rearrange("p e b f i -> p e (b f i)"),
+            )
 
-        first, second = ORDER[0], ORDER[1]
-        xr = {}
-        wraw = {}
-        for g in range(G):
-            xr[(0, g)] = load_x(0, g)
-            wraw[(first, g)] = load_w(first, g)
-        traw0 = load_tab(0)
-        for g in range(G):
-            wraw[(second, g)] = load_w(second, g)
-        for g in range(G):
-            xr[(1, g)] = load_x(1, g)
-        traw1 = load_tab(1)
-        for g in range(G):
-            wraw[(ORDER[2], g)] = load_w(ORDER[2], g)
+        okv = {}
 
-        wts = {}
-
-        def w_slice(c, g, engs):
-            if g == 0:
-                wts[c] = new_w_tiles()
-            raw = wraw[(c, g)]
-            wide = raw if c == KV else widen(g, raw)
-            group_and_quantize(g, wide, wts[c][0], wts[c][1], engs)
-
-        def head(j, units, eng):
-            accs = [new_acc() for unit in units]
-            for g in range(G):
-                prep_x(j, g, xr[(j, g)], eng)
-                if j == 0:
-                    w_slice(first, g, ("a", "p"))
-                for n, (c, q) in enumerate(units):
-                    for half in range(2):
-                        mx(wts[c], q, j, half, g, accs[n][half])
-            return accs
-
-        units = ((first, 0), (first, 1))
-        accs0 = head(0, units, "a")
-        pb = tr_pool.tile([P, P], BF16, name="pb", tag="tr")
-        nc.tensor.transpose(out=pb[:], in_=brow[:], identity=ident_b[:])
-        nc.vector.tensor_copy(out=biasT[:], in_=pb[:, 0:20])
-        build_tables(0, traw0, "p")
-        for g in range(G):
-            w_slice(second, g, W_ENGS[g])
-        pairs0 = [rope(c, q, 0, accs0[n]) for n, (c, q) in enumerate(units)]
-        accs1 = head(1, units, "a")
-        back_kv(0, pairs0)
-        build_tables(1, traw1, "p")
-        pairs1 = [rope(c, q, 1, accs1[n]) for n, (c, q) in enumerate(units)]
-        pending = []
-
-        for ci in range(1, len(ORDER)):
-            c = ORDER[ci]
-            for n, (q, j) in enumerate(((0, 0), (0, 1), (1, 0), (1, 1))):
-                accs = new_acc()
+        def kv_turn(j, b):
+            ob[(j, b)] = tr_pool.tile([P, 2, 2, P], F32, name="obkv", tag="tr")
+            for q in range(2):
                 for half in range(2):
-                    for g in range(G):
-                        mx(wts[c], q, j, half, g, accs[half])
-                if ci == 1 and n == 0:
-                    back_kv(1, pairs1)
-                for item in pending:
-                    back(item[0], item[1], item[2], item[3])
-                pending = [(c, q, j, rope(c, q, j, accs))]
-                if ci + 1 < len(ORDER):
-                    w_slice(ORDER[ci + 1], n, W_ENGS[n])
-                if ci + 2 < len(ORDER):
-                    wraw[(ORDER[ci + 2], n)] = load_w(ORDER[ci + 2], n)
-        for item in pending:
-            back(item[0], item[1], item[2], item[3])
+                    turn_back(ob[(j, b)][:, half, q, :], (KV, q, j), half, b)
+
+        def kv_out(j, b):
+            if b == 0:
+                okv[j] = o_pool.tile([P, 2, 2, 4, 2, 64], F32, name="okv", tag="okv", bufs=1)
+            nc.scalar.activation(
+                out=okv[j][:, :, :, b, :, :].rearrange("p k e f i -> p (k e) f i"),
+                in_=ob[(j, b)][:].rearrange("p f k (e i) -> p (k e) f i", e=2),
+                func=COPY,
+                scale=mk[:, 4 * j + b : 4 * j + b + 1],
+            )
+
+        def kv_store(j):
+            for q in range(2):
+                nc.sync.dma_start(out=out_v[1 + q][j], in_=okv[j][:, q].rearrange("p e b f i -> p e (b f i)"))
+
+        k0, v0, k1, v1 = (KV, 0, 0), (KV, 1, 0), (KV, 0, 1), (KV, 1, 1)
+        units = [(c, q, j) for c in range(4) for j in range(2) for q in range(2)]
+        slices = [(c, g) for c in range(4) for g in range(G)]
+
+        def widen(s):
+            if s < 16:
+                w_widen(slices[s][0], slices[s][1])
+
+        def group(s, engs):
+            if s < 16:
+                w_group(slices[s][0], slices[s][1], engs)
+
+        def quant(s):
+            if s < 16:
+                w_quant(slices[s][0], slices[s][1])
+
+        def mx_pass(pair, g):
+            for unit in pair:
+                for half in range(2):
+                    mx(unit, half, g)
+
+        def finish_kv(j):
+            for b in range(4):
+                kv_turn(j, b)
+                kv_out(j, b)
+            kv_store(j)
+
+        def finish(unit):
+            for half in range(2):
+                back_turn(unit, half)
+                back_out(unit, half)
+            back_store(unit)
+
+        for g in range(G):
+            load_x(0, g)
+            load_w(KV, g)
+            if g == 1:
+                load_tab(0)
+        load_wsc()
+        for g in range(G):
+            load_w(0, g)
+        load_bias(0)
+        load_bias(1)
+        load_mask()
+        for g in range(2):
+            load_x(1, g)
+
+        def first_prep(g):
+            x_out(0, g, "aa")
+            w_group(KV, g, ("a", "v"))
+            x_quant(0, g)
+            w_quant(KV, g)
+
+        x_turn(0, 0)
+        first_prep(0)
+        x_turn(0, 1)
+        load_x(1, 2)
+        first_prep(1)
+        mx_pass((v0, k0), 0)
+        x_turn(0, 2)
+        load_x(1, 3)
+        load_tab(1)
+        for c in range(1, 4):
+            for g in range(G):
+                load_w(c, g)
+        tab_gather(0, 0, "p")
+        tab_gather(0, 1, "p")
+        first_prep(2)
+        mx_pass((v0, k0), 1)
+        x_turn(0, 3)
+        first_prep(3)
+        mx_pass((v0, k0), 2)
+        tab_turn(0, 0, "v")
+        tab_turn(0, 1, "v")
+        bias_turn()
+        mx_pass((v0, k0), 3)
+
+        widen(0)
+        group(0, ("a", "p"))
+        widen(1)
+        group(1, ("a", "p"))
+        rope(v0, 0)
+        rope(v0, 1)
+        x_turn(1, 0)
+        x_turn(1, 1)
+        rope(k0, 0)
+        rope(k0, 1)
+        x_out(1, 0, "vv")
+        x_quant(1, 0)
+        x_out(1, 1, "vv")
+        x_quant(1, 1)
+        x_turn(1, 2)
+        x_turn(1, 3)
+        tab_gather(1, 0, "p")
+        tab_gather(1, 1, "p")
+        widen(2)
+        group(2, ("p", "p"))
+        x_out(1, 2, "vv")
+        x_quant(1, 2)
+        quant(0)
+        x_out(1, 3, "vv")
+        x_quant(1, 3)
+        quant(1)
+        tab_turn(1, 0, "v")
+        tab_turn(1, 1, "v")
+        for g in range(G):
+            mx_pass((v1, k1), g)
+        widen(3)
+        group(3, ("p", "p"))
+        widen(4)
+        quant(2)
+        finish_kv(0)
+        rope(v1, 0)
+        rope(v1, 1)
+        group(4, ("p", "p"))
+        quant(3)
+        rope(k1, 0)
+        rope(k1, 1)
+        widen(5)
+
+        for n, unit in enumerate(units):
+            for half in range(2):
+                for g in range(G):
+                    mx(unit, half, g)
+            widen(n + 6)
+            if n == 0:
+                finish_kv(1)
+            else:
+                finish(units[n - 1])
+            rope(unit, 0)
+            quant(n + 4)
+            rope(unit, 1)
+            group(n + 5, ("p", "p"))
+            if n >= 12:
+                add_on("p", unit, 0)
+                add_on("p", unit, 1)
+        finish(units[-1])

@@ -37,8 +37,8 @@ def tile_multiheadattention_pa_kernel(
     with ExitStack() as ctx:
         const = ctx.enter_context(tc.tile_pool(name="const", bufs=1))
         xr_pool = ctx.enter_context(tc.tile_pool(name="xr_pool", bufs=6))
-        wb_pool = ctx.enter_context(tc.tile_pool(name="wb_pool", bufs=16))
-        kv_pool = ctx.enter_context(tc.tile_pool(name="kv_pool", bufs=4))
+        wb_pool = ctx.enter_context(tc.tile_pool(name="wb_pool", bufs=8))
+        kv_pool = ctx.enter_context(tc.tile_pool(name="kv_pool", bufs=8))
         tb_pool = ctx.enter_context(tc.tile_pool(name="tb_pool", bufs=4))
         wc_pool = ctx.enter_context(tc.tile_pool(name="wc_pool", bufs=3))
         xg_pool = ctx.enter_context(tc.tile_pool(name="xg_pool", bufs=2))
@@ -85,16 +85,15 @@ def tile_multiheadattention_pa_kernel(
             xr[(j, g)] = xr_pool.tile([P, 4, 512], BF16, name="xr", tag="xr")
             nc.sync.dma_start(out=xr[(j, g)][:], in_=x_v[j, g])
 
-        def load_w(c, g):
-            if c == KV:
-                kvraw = kv_pool.tile([P, 4, 512], BF16, name="kvraw", tag="kvraw")
-                nc.sync.dma_start(out=kvraw[:, :, 0:256], in_=wk_v[g])
-                nc.sync.dma_start(out=kvraw[:, :, 256:512], in_=wv_v[g])
-                wraw[(c, g)] = kvraw
-            else:
-                wq_sb = wb_pool.tile([P, 4, 512], U8, name="wq_sb", tag="wq_sb")
-                nc.sync.dma_start(out=wq_sb[:], in_=wq_v[g][:, :, c * 512 : (c + 1) * 512])
-                wraw[(c, g)] = wq_sb
+        def load_kv(g):
+            for m, view in enumerate((wk_v, wv_v)):
+                wraw[(KV, g, m)] = kv_pool.tile([P, 4, 256], BF16, name="kvraw", tag="kvraw")
+                nc.sync.dma_start(out=wraw[(KV, g, m)][:], in_=view[g])
+
+        def load_wq(pair, g):
+            wq_sb = wb_pool.tile([P, 4, 1024], U8, name="wq_sb", tag="wq_sb")
+            nc.sync.dma_start(out=wq_sb[:], in_=wq_v[g][:, :, pair * 1024 : (pair + 1) * 1024])
+            wraw[(pair, g)] = wq_sb
 
         def load_tab(j):
             for a in range(2):
@@ -154,18 +153,30 @@ def tile_multiheadattention_pa_kernel(
             for t in range(4):
                 nc.scalar.activation(
                     out=wide[(c, g)][:, t, :],
-                    in_=wraw[(c, g)][:, t, :].bitcast(FP8),
+                    in_=wraw[(c // 2, g)][:, t, (c % 2) * 512 : (c % 2 + 1) * 512].bitcast(FP8),
                     func=COPY,
                     scale=wsc[:, 4 * g + t : 4 * g + t + 1],
                 )
 
         def w_group(c, g, engs):
             grp[(c, g)] = grp_pool.tile([P, 2048], BF16, name="grp", tag="grp", align_bytes=64)
-            source = wraw[(c, g)] if c == KV else wide[(c, g)]
             dst = grp[(c, g)][:].rearrange("p (f h i t) -> p f h i t", f=2, h=4, i=64)
-            src = source[:].rearrange("p t (h f i) -> p f h i t", h=4, f=2)
-            for half in range(2):
-                copy_on(engs[half], dst[:, half], src[:, half])
+            if c == KV:
+                for m in range(2):
+                    src = wraw[(KV, g, m)][:].rearrange("p t (h f i) -> p f h i t", h=2, f=2)
+                    for half in range(2):
+                        copy_on(engs[half], dst[:, half, 2 * m : 2 * m + 2], src[:, half])
+            else:
+                src = wide[(c, g)][:].rearrange("p t (h f i) -> p f h i t", h=4, f=2)
+                if engs[0] == engs[1]:
+                    copy_on(
+                        engs[0],
+                        grp[(c, g)][:].rearrange("p (f h i t) -> p h f i t", f=2, h=4, i=64),
+                        wide[(c, g)][:].rearrange("p t (h f i) -> p h f i t", h=4, f=2),
+                    )
+                else:
+                    for half in range(2):
+                        copy_on(engs[half], dst[:, half], src[:, half])
 
         def w_quant(c, g):
             if g == 0:
@@ -347,12 +358,12 @@ def tile_multiheadattention_pa_kernel(
 
         for g in range(G):
             load_x(0, g)
-            load_w(KV, g)
+            load_kv(g)
             if g == 1:
                 load_tab(0)
         load_wsc()
-        for g in range(G):
-            load_w(0, g)
+        load_wq(0, 0)
+        load_wq(0, 1)
         load_bias(0)
         load_bias(1)
         load_mask()
@@ -373,10 +384,11 @@ def tile_multiheadattention_pa_kernel(
         mx_pass((v0, k0), 0)
         x_turn(0, 2)
         load_x(1, 3)
+        load_wq(0, 2)
+        load_wq(0, 3)
         load_tab(1)
-        for c in range(1, 4):
-            for g in range(G):
-                load_w(c, g)
+        for g in range(G):
+            load_wq(1, g)
         tab_gather(0, 0, "p")
         tab_gather(0, 1, "p")
         first_prep(2)

@@ -150,12 +150,22 @@ def tile_multiheadattention_pa_kernel(
 
         def w_widen(c, g):
             wide[(c, g)] = wide_pool.tile([P, 4, 512], BF16, name="wide", tag="wide")
-            for t in range(4):
+            for t in range(3):
                 nc.scalar.activation(
                     out=wide[(c, g)][:, t, :],
                     in_=wraw[(c // 2, g)][:, t, (c % 2) * 512 : (c % 2 + 1) * 512].bitcast(FP8),
                     func=COPY,
                     scale=wsc[:, 4 * g + t : 4 * g + t + 1],
+                )
+
+        def w_widen_v(c, g):
+            for t in range(3, 4):
+                nc.vector.tensor_scalar(
+                    out=wide[(c, g)][:, t, :],
+                    in0=wraw[(c // 2, g)][:, t, (c % 2) * 512 : (c % 2 + 1) * 512].bitcast(FP8),
+                    scalar1=wsc[:, 4 * g + t : 4 * g + t + 1],
+                    scalar2=None,
+                    op0=MULT,
                 )
 
         def w_group(c, g, engs):
@@ -331,6 +341,10 @@ def tile_multiheadattention_pa_kernel(
             if s < 16:
                 w_widen(slices[s][0], slices[s][1])
 
+        def widen_v(s):
+            if s < 16:
+                w_widen_v(slices[s][0], slices[s][1])
+
         def group(s, engs):
             if s < 16:
                 w_group(slices[s][0], slices[s][1], engs)
@@ -402,8 +416,10 @@ def tile_multiheadattention_pa_kernel(
         mx_pass((v0, k0), 3)
 
         widen(0)
+        widen_v(0)
         group(0, ("a", "p"))
         widen(1)
+        widen_v(1)
         group(1, ("a", "p"))
         rope(v0, 0)
         rope(v0, 1)
@@ -420,6 +436,7 @@ def tile_multiheadattention_pa_kernel(
         tab_gather(1, 0, "p")
         tab_gather(1, 1, "p")
         widen(2)
+        widen_v(2)
         group(2, ("p", "p"))
         x_out(1, 2, "vv")
         x_quant(1, 2)
@@ -432,8 +449,10 @@ def tile_multiheadattention_pa_kernel(
         for g in range(G):
             mx_pass((v1, k1), g)
         widen(3)
+        widen_v(3)
         group(3, ("p", "p"))
         widen(4)
+        widen_v(4)
         quant(2)
         finish_kv(0)
         rope(v1, 0)
@@ -443,6 +462,7 @@ def tile_multiheadattention_pa_kernel(
         rope(k1, 0)
         rope(k1, 1)
         widen(5)
+        widen_v(5)
 
         for n, unit in enumerate(units):
             for half in range(2):
@@ -455,6 +475,7 @@ def tile_multiheadattention_pa_kernel(
                 finish(units[n - 1])
             rope(unit, 0)
             quant(n + 4)
+            widen_v(n + 6)
             rope(unit, 1)
             group(n + 5, ("p", "p"))
             if n >= 12:

@@ -150,22 +150,12 @@ def tile_multiheadattention_pa_kernel(
 
         def w_widen(c, g):
             wide[(c, g)] = wide_pool.tile([P, 4, 512], BF16, name="wide", tag="wide")
-            for t in range(3):
+            for t in range(4):
                 nc.scalar.activation(
                     out=wide[(c, g)][:, t, :],
                     in_=wraw[(c // 2, g)][:, t, (c % 2) * 512 : (c % 2 + 1) * 512].bitcast(FP8),
                     func=COPY,
                     scale=wsc[:, 4 * g + t : 4 * g + t + 1],
-                )
-
-        def w_widen_v(c, g):
-            for t in range(3, 4):
-                nc.vector.tensor_scalar(
-                    out=wide[(c, g)][:, t, :],
-                    in0=wraw[(c // 2, g)][:, t, (c % 2) * 512 : (c % 2 + 1) * 512].bitcast(FP8),
-                    scalar1=wsc[:, 4 * g + t : 4 * g + t + 1],
-                    scalar2=None,
-                    op0=MULT,
                 )
 
         def w_group(c, g, engs):
@@ -178,15 +168,8 @@ def tile_multiheadattention_pa_kernel(
                         copy_on(engs[half], dst[:, half, 2 * m : 2 * m + 2], src[:, half])
             else:
                 src = wide[(c, g)][:].rearrange("p t (h f i) -> p f h i t", h=4, f=2)
-                if engs[0] == engs[1]:
-                    copy_on(
-                        engs[0],
-                        grp[(c, g)][:].rearrange("p (f h i t) -> p h f i t", f=2, h=4, i=64),
-                        wide[(c, g)][:].rearrange("p t (h f i) -> p h f i t", h=4, f=2),
-                    )
-                else:
-                    for half in range(2):
-                        copy_on(engs[half], dst[:, half], src[:, half])
+                for half in range(2):
+                    copy_on(engs[half], dst[:, half], src[:, half])
 
         def w_quant(c, g):
             if g == 0:
@@ -341,10 +324,6 @@ def tile_multiheadattention_pa_kernel(
             if s < 16:
                 w_widen(slices[s][0], slices[s][1])
 
-        def widen_v(s):
-            if s < 16:
-                w_widen_v(slices[s][0], slices[s][1])
-
         def group(s, engs):
             if s < 16:
                 w_group(slices[s][0], slices[s][1], engs)
@@ -416,10 +395,8 @@ def tile_multiheadattention_pa_kernel(
         mx_pass((v0, k0), 3)
 
         widen(0)
-        widen_v(0)
         group(0, ("a", "p"))
         widen(1)
-        widen_v(1)
         group(1, ("a", "p"))
         rope(v0, 0)
         rope(v0, 1)
@@ -436,7 +413,6 @@ def tile_multiheadattention_pa_kernel(
         tab_gather(1, 0, "p")
         tab_gather(1, 1, "p")
         widen(2)
-        widen_v(2)
         group(2, ("p", "p"))
         x_out(1, 2, "vv")
         x_quant(1, 2)
@@ -449,10 +425,8 @@ def tile_multiheadattention_pa_kernel(
         for g in range(G):
             mx_pass((v1, k1), g)
         widen(3)
-        widen_v(3)
         group(3, ("p", "p"))
         widen(4)
-        widen_v(4)
         quant(2)
         finish_kv(0)
         rope(v1, 0)
@@ -462,7 +436,6 @@ def tile_multiheadattention_pa_kernel(
         rope(k1, 0)
         rope(k1, 1)
         widen(5)
-        widen_v(5)
 
         for n, unit in enumerate(units):
             for half in range(2):
@@ -475,10 +448,11 @@ def tile_multiheadattention_pa_kernel(
                 finish(units[n - 1])
             rope(unit, 0)
             quant(n + 4)
-            widen_v(n + 6)
             rope(unit, 1)
             group(n + 5, ("p", "p"))
             if n >= 12:
                 add_on("p", unit, 0)
                 add_on("p", unit, 1)
+            else:
+                add_on("v", unit, 1)
         finish(units[-1])

@@ -16,9 +16,16 @@ IDENT = mybir.ActivationFunctionType.Identity
 
 FLOPS = 2 * 1024 * 2048 * 2560
 
+WCB = 5
+WIDEB = 6
+GRPB = 4
+UWB = 3
+OKVB = 1
+WBB = {2: 8, 4: 4}
 P = 128
 G = 4
-KV = 4
+KP = 8
+VP = 9
 SECTIONS = ((0, 0, 16), (1, 16, 24), (2, 40, 24))
 
 
@@ -29,8 +36,7 @@ def tile_multiheadattention_pa_kernel(
 
     x_v = x[0].rearrange("(j r b) (g k) -> j g r b k", j=2, r=P, b=4, g=G)
     wq_v = Wq_bytes.rearrange("(g p t) n -> g p t n", g=G, p=P, t=4)
-    wk_v = Wk.rearrange("(g p t) n -> g p t n", g=G, p=P, t=4)
-    wv_v = Wv.rearrange("(g p t) n -> g p t n", g=G, p=P, t=4)
+    wkv_v = [a.rearrange("(g p t) n -> g p t n", g=G, p=P, t=4) for a in (Wk, Wv)]
     tab_v = [a[:, 0].rearrange("t (j r b) d -> j r t (b d)", j=2, r=P, b=4) for a in (cos, sin)]
     out_v = [a[0].rearrange("h (j r b) d -> j r h (b d)", j=2, r=P, b=4) for a in (out_0, out_1, out_2)]
 
@@ -40,11 +46,11 @@ def tile_multiheadattention_pa_kernel(
         wb_pool = ctx.enter_context(tc.tile_pool(name="wb_pool", bufs=8))
         kv_pool = ctx.enter_context(tc.tile_pool(name="kv_pool", bufs=8))
         tb_pool = ctx.enter_context(tc.tile_pool(name="tb_pool", bufs=4))
-        wc_pool = ctx.enter_context(tc.tile_pool(name="wc_pool", bufs=3))
+        wc_pool = ctx.enter_context(tc.tile_pool(name="wc_pool", bufs=WCB))
         xg_pool = ctx.enter_context(tc.tile_pool(name="xg_pool", bufs=2))
-        wide_pool = ctx.enter_context(tc.tile_pool(name="wide_pool", bufs=3))
-        grp_pool = ctx.enter_context(tc.tile_pool(name="grp_pool", bufs=3))
-        uw_pool = ctx.enter_context(tc.tile_pool(name="uw_pool", bufs=3))
+        wide_pool = ctx.enter_context(tc.tile_pool(name="wide_pool", bufs=WIDEB))
+        grp_pool = ctx.enter_context(tc.tile_pool(name="grp_pool", bufs=GRPB))
+        uw_pool = ctx.enter_context(tc.tile_pool(name="uw_pool", bufs=UWB))
         o_pool = ctx.enter_context(tc.tile_pool(name="o_pool", bufs=3))
         acc_pool = ctx.enter_context(tc.psum_pool(name="acc_pool", bufs=4))
         tr_pool = ctx.enter_context(tc.psum_pool(name="tr_pool", bufs=4))
@@ -86,36 +92,38 @@ def tile_multiheadattention_pa_kernel(
             nc.sync.dma_start(out=xr[(j, g)][:], in_=x_v[j, g])
 
         def load_kv(g):
-            for m, view in enumerate((wk_v, wv_v)):
-                wraw[(KV, g, m)] = kv_pool.tile([P, 4, 256], BF16, name="kvraw", tag="kvraw")
-                nc.sync.dma_start(out=wraw[(KV, g, m)][:], in_=view[g])
+            for m in range(2):
+                kvraw = kv_pool.tile([P, 4, 256], BF16, name="kvraw", tag="kvraw")
+                nc.sync.dma_start(out=kvraw[:], in_=wkv_v[m][g])
+                wraw[(KP + m, g)] = (kvraw, 0)
 
-        def load_wq(pair, g):
-            wq_sb = wb_pool.tile([P, 4, 1024], U8, name="wq_sb", tag="wq_sb")
-            nc.sync.dma_start(out=wq_sb[:], in_=wq_v[g][:, :, pair * 1024 : (pair + 1) * 1024])
-            wraw[(pair, g)] = wq_sb
+        def load_wq(hp0, n, g):
+            wq_sb = wb_pool.tile([P, 4, n * 256], U8, name="wq_sb%d" % n, tag="wq_sb%d" % n, bufs=WBB[n])
+            nc.sync.dma_start(out=wq_sb[:], in_=wq_v[g][:, :, hp0 * 256 : (hp0 + n) * 256])
+            for i in range(n):
+                wraw[(hp0 + i, g)] = (wq_sb, i)
 
         def load_tab(j):
             for a in range(2):
                 traw[(j, a)] = tb_pool.tile([P, 3, 512], BF16, name="traw", tag="traw")
                 nc.sync.dma_start(out=traw[(j, a)][:], in_=tab_v[a][j])
 
-        def load_wsc():
-            nc.sync.dma_start(
+        def load_wsc(eng):
+            eng.dma_start(
                 out=wsc[:].rearrange("p (g t) -> p g t", t=4),
                 in_=Wq_scale.rearrange("(g p t) o -> p g (t o)", g=G, p=P, t=4),
             )
 
-        def load_mask():
-            nc.sync.dma_start(
+        def load_mask(eng):
+            eng.dma_start(
                 out=mk_b[:].rearrange("p (j b) -> p j b", b=4),
                 in_=mask[0].rearrange("(j r b) -> r j b", j=2, r=P, b=4),
             )
 
-        def load_bias(half):
+        def load_bias(half, eng):
             for vec, row, n in ((bq, 0, 8), (bk, 8, 1), (bv, 9, 1)):
                 r0 = half * 10 + row
-                nc.sync.dma_start(
+                eng.dma_start(
                     out=brow[r0 : r0 + n, :].rearrange("h (e i) -> h e i", e=2),
                     in_=vec.rearrange("(h e f i) -> f h e i", e=2, f=2, i=64)[half],
                 )
@@ -148,36 +156,34 @@ def tile_multiheadattention_pa_kernel(
         grp = {}
         wts = {}
 
-        def w_widen(c, g):
-            wide[(c, g)] = wide_pool.tile([P, 4, 512], BF16, name="wide", tag="wide")
+        def w_widen(hp, g):
+            wide[(hp, g)] = wide_pool.tile([P, 4, 256], BF16, name="wide", tag="wide")
+            raw, i = wraw[(hp, g)]
             for t in range(4):
                 nc.scalar.activation(
-                    out=wide[(c, g)][:, t, :],
-                    in_=wraw[(c // 2, g)][:, t, (c % 2) * 512 : (c % 2 + 1) * 512].bitcast(FP8),
+                    out=wide[(hp, g)][:, t, :],
+                    in_=raw[:, t, i * 256 : (i + 1) * 256].bitcast(FP8),
                     func=COPY,
                     scale=wsc[:, 4 * g + t : 4 * g + t + 1],
                 )
 
-        def w_group(c, g, engs):
-            grp[(c, g)] = grp_pool.tile([P, 2048], BF16, name="grp", tag="grp", align_bytes=64)
-            dst = grp[(c, g)][:].rearrange("p (f h i t) -> p f h i t", f=2, h=4, i=64)
-            if c == KV:
-                for m in range(2):
-                    src = wraw[(KV, g, m)][:].rearrange("p t (h f i) -> p f h i t", h=2, f=2)
-                    for half in range(2):
-                        copy_on(engs[half], dst[:, half, 2 * m : 2 * m + 2], src[:, half])
+        def w_group(hp, g, engs):
+            grp[(hp, g)] = grp_pool.tile([P, 1024], BF16, name="grp", tag="grp", align_bytes=64)
+            dst = grp[(hp, g)][:].rearrange("p (f e i t) -> p f e i t", f=2, e=2, i=64)
+            src = (wide[(hp, g)] if hp < KP else wraw[(hp, g)][0])[:].rearrange("p t (e f i) -> p f e i t", e=2, f=2)
+            if len(engs) == 1:
+                copy_on(engs, dst, src)
             else:
-                src = wide[(c, g)][:].rearrange("p t (h f i) -> p f h i t", h=4, f=2)
                 for half in range(2):
                     copy_on(engs[half], dst[:, half], src[:, half])
 
-        def w_quant(c, g):
+        def w_quant(hp, g):
             if g == 0:
-                codes = wc_pool.tile([P, G, 512], U32, name="w_codes", tag="w_codes", align_bytes=64)
-                scales = wc_pool.tile([P, G, 512], U8, name="w_scales", tag="w_scales", align_bytes=64)
-                wts[c] = (codes, scales)
+                codes = wc_pool.tile([P, G, 256], U32, name="w_codes", tag="w_codes", align_bytes=64)
+                scales = wc_pool.tile([P, G, 256], U8, name="w_scales", tag="w_scales", align_bytes=64)
+                wts[hp] = (codes, scales)
             nc.vector.quantize_mx(
-                out=wts[c][0][:, g, :].bitcast(FP8X4), scales=wts[c][1][:, g, :], in_=grp[(c, g)][:]
+                out=wts[hp][0][:, g, :].bitcast(FP8X4), scales=wts[hp][1][:, g, :], in_=grp[(hp, g)][:]
             )
 
         asm = {}
@@ -217,29 +223,31 @@ def tile_multiheadattention_pa_kernel(
         summed = set()
 
         def mx(unit, half, g):
-            c, q, j = unit
+            hp, j = unit
             if g == 0:
                 accs[(unit, half)] = acc_pool.tile([P, 512], F32, name="acc", tag="acc")
-            cols = slice((half * 2 + q) * P, (half * 2 + q + 1) * P)
+            cols = slice(half * P, (half + 1) * P)
             nc.tensor.matmul_mx(
                 out=accs[(unit, half)][:],
-                lhsT=wts[c][0][:, g, cols].bitcast(FP8X4),
-                lhsT_scale=wts[c][1][:, g, cols],
+                lhsT=wts[hp][0][:, g, cols].bitcast(FP8X4),
+                lhsT_scale=wts[hp][1][:, g, cols],
                 rhs=x_codes[:, g, j, :].bitcast(FP8X4),
                 rhs_scale=x_scales[:, g, j, :],
                 start=(g == 0),
                 stop=(g == G - 1),
             )
 
-        def rope(unit, half):
-            c, q, j = unit
-            hp = 2 * c + q
+        def rope(unit, half, eng="v"):
+            hp, j = unit
             bias = biasT[:, 10 * half + hp : 10 * half + hp + 1]
             acc = accs[(unit, half)]
-            if hp == 9:
+            if hp == VP:
                 name = ("u_lo", "u_hi")[half]
                 uw[(unit, name)] = uw_pool.tile([P, 512], F32, name=name, tag=name)
-                nc.vector.tensor_scalar(out=uw[(unit, name)][:], in0=acc[:], scalar1=bias, scalar2=None, op0=ADD)
+                if eng == "a":
+                    nc.scalar.activation(out=uw[(unit, name)][:], in_=acc[:], func=IDENT, bias=bias)
+                else:
+                    nc.vector.tensor_scalar(out=uw[(unit, name)][:], in0=acc[:], scalar1=bias, scalar2=None, op0=ADD)
                 return
             for name, k in ((("u_lo", 0), ("w_hi", 3)), (("w_lo", 2), ("u_hi", 1)))[half]:
                 uw[(unit, name)] = uw_pool.tile([P, 512], F32, name=name, tag=name)
@@ -288,9 +296,9 @@ def tile_multiheadattention_pa_kernel(
             )
 
         def back_store(unit):
-            c, q, j = unit
+            hp, j = unit
             nc.sync.dma_start(
-                out=out_v[0][j][:, 4 * c + 2 * q : 4 * c + 2 * q + 2, :],
+                out=out_v[0][j][:, 2 * hp : 2 * hp + 2, :],
                 in_=o_sb[unit][:].rearrange("p e b f i -> p e (b f i)"),
             )
 
@@ -300,11 +308,11 @@ def tile_multiheadattention_pa_kernel(
             ob[(j, b)] = tr_pool.tile([P, 2, 2, P], F32, name="obkv", tag="tr")
             for q in range(2):
                 for half in range(2):
-                    turn_back(ob[(j, b)][:, half, q, :], (KV, q, j), half, b)
+                    turn_back(ob[(j, b)][:, half, q, :], (KP + q, j), half, b)
 
         def kv_out(j, b):
             if b == 0:
-                okv[j] = o_pool.tile([P, 2, 2, 4, 2, 64], F32, name="okv", tag="okv", bufs=1)
+                okv[j] = o_pool.tile([P, 2, 2, 4, 2, 64], F32, name="okv", tag="okv", bufs=OKVB)
             nc.scalar.activation(
                 out=okv[j][:, :, :, b, :, :].rearrange("p k e f i -> p (k e) f i"),
                 in_=ob[(j, b)][:].rearrange("p f k (e i) -> p (k e) f i", e=2),
@@ -316,25 +324,14 @@ def tile_multiheadattention_pa_kernel(
             for q in range(2):
                 nc.sync.dma_start(out=out_v[1 + q][j], in_=okv[j][:, q].rearrange("p e b f i -> p e (b f i)"))
 
-        k0, v0, k1, v1 = (KV, 0, 0), (KV, 1, 0), (KV, 0, 1), (KV, 1, 1)
-        units = [(c, q, j) for c in range(4) for j in range(2) for q in range(2)]
-        slices = [(c, g) for c in range(4) for g in range(G)]
-
-        def widen(s):
-            if s < 16:
-                w_widen(slices[s][0], slices[s][1])
-
-        def group(s, engs):
-            if s < 16:
-                w_group(slices[s][0], slices[s][1], engs)
-
-        def quant(s):
-            if s < 16:
-                w_quant(slices[s][0], slices[s][1])
-
         def mx_pass(pair, g):
             for unit in pair:
                 for half in range(2):
+                    mx(unit, half, g)
+
+        def mx_all(unit):
+            for half in range(2):
+                for g in range(G):
                     mx(unit, half, g)
 
         def finish_kv(j):
@@ -349,110 +346,147 @@ def tile_multiheadattention_pa_kernel(
                 back_out(unit, half)
             back_store(unit)
 
-        for g in range(G):
-            load_x(0, g)
-            load_kv(g)
-            if g == 1:
-                load_tab(0)
-        load_wsc()
-        load_wq(0, 0)
-        load_wq(0, 1)
-        load_bias(0)
-        load_bias(1)
-        load_mask()
-        for g in range(2):
-            load_x(1, g)
+        k0, v0, k1, v1 = (KP, 0), (VP, 0), (KP, 1), (VP, 1)
+        sl = [(hp, g) for hp in range(8) for g in range(G)]
+
+        def widen(s):
+            if s < 32:
+                w_widen(sl[s][0], sl[s][1])
+
+        def group(s, engs):
+            if s < 32:
+                w_group(sl[s][0], sl[s][1], engs)
+
+        def quant(s):
+            if s < 32:
+                w_quant(sl[s][0], sl[s][1])
+
+        load_wsc(nc.gpsimd)
+        load_bias(0, nc.gpsimd)
+        load_bias(1, nc.gpsimd)
+        load_mask(nc.gpsimd)
+        load_x(0, 0)
+        load_kv(0)
+        load_x(0, 1)
+        load_kv(1)
+        load_wq(0, 2, 0)
+        load_wq(0, 2, 1)
+        load_x(0, 2)
+        load_kv(2)
+        load_x(0, 3)
+        load_kv(3)
+        load_tab(0)
+        load_wq(0, 2, 2)
+        load_wq(0, 2, 3)
+        load_x(1, 0)
+        load_x(1, 1)
 
         def first_prep(g):
             x_out(0, g, "aa")
-            w_group(KV, g, ("a", "v"))
+            w_group(KP, g, "vv")
+            w_group(VP, g, "vv")
             x_quant(0, g)
-            w_quant(KV, g)
+            w_quant(KP, g)
+            w_quant(VP, g)
 
         x_turn(0, 0)
         first_prep(0)
         x_turn(0, 1)
         load_x(1, 2)
         first_prep(1)
+        widen(0)
+        widen(1)
         mx_pass((v0, k0), 0)
         x_turn(0, 2)
         load_x(1, 3)
-        load_wq(0, 2)
-        load_wq(0, 3)
+        for g in range(G):
+            load_wq(2, 2, g)
         load_tab(1)
         for g in range(G):
-            load_wq(1, g)
-        tab_gather(0, 0, "p")
-        tab_gather(0, 1, "p")
+            load_wq(4, 4, g)
         first_prep(2)
         mx_pass((v0, k0), 1)
         x_turn(0, 3)
         first_prep(3)
+        widen(4)
+        widen(5)
         mx_pass((v0, k0), 2)
-        tab_turn(0, 0, "v")
-        tab_turn(0, 1, "v")
+        tab_gather(0, 0, "a")
+        tab_gather(0, 1, "a")
         bias_turn()
         mx_pass((v0, k0), 3)
-
-        widen(0)
-        group(0, ("a", "p"))
-        widen(1)
-        group(1, ("a", "p"))
+        group(0, "vv")
+        group(1, "vv")
+        quant(0)
+        quant(1)
+        widen(2)
+        widen(3)
         rope(v0, 0)
         rope(v0, 1)
         x_turn(1, 0)
+        x_out(1, 0, "aa")
+        group(2, "vv")
+        group(3, "vv")
+        quant(2)
+        quant(3)
+        mx_all((0, 0))
+        tab_turn(0, 0, "v")
+        tab_turn(0, 1, "v")
         x_turn(1, 1)
+        x_out(1, 1, "aa")
+        widen(6)
+        widen(7)
         rope(k0, 0)
         rope(k0, 1)
-        x_out(1, 0, "vv")
         x_quant(1, 0)
-        x_out(1, 1, "vv")
         x_quant(1, 1)
-        x_turn(1, 2)
-        x_turn(1, 3)
-        tab_gather(1, 0, "p")
-        tab_gather(1, 1, "p")
-        widen(2)
-        group(2, ("p", "p"))
-        x_out(1, 2, "vv")
-        x_quant(1, 2)
-        quant(0)
-        x_out(1, 3, "vv")
-        x_quant(1, 3)
-        quant(1)
-        tab_turn(1, 0, "v")
-        tab_turn(1, 1, "v")
-        for g in range(G):
-            mx_pass((v1, k1), g)
-        widen(3)
-        group(3, ("p", "p"))
-        widen(4)
-        quant(2)
-        finish_kv(0)
-        rope(v1, 0)
-        rope(v1, 1)
-        group(4, ("p", "p"))
-        quant(3)
-        rope(k1, 0)
-        rope(k1, 1)
-        widen(5)
+        group(4, "vv")
+        group(5, "vv")
+        quant(4)
+        quant(5)
 
-        for n, unit in enumerate(units):
-            for half in range(2):
-                for g in range(G):
-                    mx(unit, half, g)
-            widen(n + 6)
-            if n == 0:
+        order = [(0, 0), (1, 0), v1, k1, (0, 1), (1, 1)] + [(hp, j) for hp in range(2, 8) for j in range(2)]
+        prev = None
+        for m, unit in enumerate(order):
+            if m > 0:
+                mx_all(unit)
+            if m == 0:
+                x_turn(1, 2)
+                x_out(1, 2, "aa")
+                x_turn(1, 3)
+                x_out(1, 3, "aa")
+                group(6, "vv")
+                group(7, "vv")
+                quant(6)
+                quant(7)
+            widen(2 * m + 8)
+            widen(2 * m + 9)
+            if m == 0:
+                finish_kv(0)
+            elif unit == k1:
+                pass
+            elif prev == k1:
                 finish_kv(1)
             else:
-                finish(units[n - 1])
+                finish(prev)
+            if m == 0:
+                x_quant(1, 2)
+                x_quant(1, 3)
+            if m == 1:
+                tab_gather(1, 0, "p")
+                tab_gather(1, 1, "p")
+            if m == 2:
+                tab_turn(1, 0, "v")
+                tab_turn(1, 1, "v")
             rope(unit, 0)
-            quant(n + 4)
+            if m >= 2:
+                quant(2 * m + 4)
+                quant(2 * m + 5)
             rope(unit, 1)
-            group(n + 5, ("p", "p"))
-            if n >= 12:
-                add_on("p", unit, 0)
-                add_on("p", unit, 1)
-            else:
+            if m >= 1:
+                group(2 * m + 6, "pp")
+                group(2 * m + 7, "aa" if m % 4 == 0 else "pp")
+            if unit[0] < KP and m < 17:
                 add_on("v", unit, 1)
-        finish(units[-1])
+            prev = unit if unit != v1 else prev
+        finish(order[-1])

@@ -375,9 +375,9 @@ def tile_multiheadattention_pa_kernel(
         load_kv(2)
         load_x(0, 3)
         load_kv(3)
-        load_tab(0)
         load_wq(0, 2, 2)
         load_wq(0, 2, 3)
+        load_tab(0)
         load_x(1, 0)
         load_x(1, 1)
 
@@ -408,8 +408,8 @@ def tile_multiheadattention_pa_kernel(
         mx_pass((v0, k0), 1)
         x_turn(0, 3)
         first_prep(3)
-        widen(4)
-        widen(5)
+        widen(2)
+        widen(3)
         mx_pass((v0, k0), 2)
         tab_gather(0, 0, "a")
         tab_gather(0, 1, "a")
@@ -419,12 +419,12 @@ def tile_multiheadattention_pa_kernel(
         group(1, "vv")
         quant(0)
         quant(1)
-        widen(2)
-        widen(3)
         rope(v0, 0)
         rope(v0, 1)
         x_turn(1, 0)
         x_out(1, 0, "aa")
+        widen(4)
+        widen(5)
         group(2, "vv")
         group(3, "vv")
         quant(2)

@@ -486,7 +486,7 @@ def tile_multiheadattention_pa_kernel(
             if m >= 1:
                 group(2 * m + 6, "pp")
                 group(2 * m + 7, "aa" if m % 4 == 0 else "pp")
-            if unit[0] < KP and m < 17:
+            if unit[0] < KP and m % 2 == 0:
                 add_on("v", unit, 1)
             prev = unit if unit != v1 else prev
         finish(order[-1])

@@ -479,14 +479,14 @@ def tile_multiheadattention_pa_kernel(
                 tab_turn(1, 0, "v")
                 tab_turn(1, 1, "v")
             rope(unit, 0)
-            if m >= 2:
-                quant(2 * m + 4)
-                quant(2 * m + 5)
             rope(unit, 1)
             if m >= 1:
                 group(2 * m + 6, "pp")
                 group(2 * m + 7, "aa" if m % 4 == 0 else "pp")
             if unit[0] < KP and m % 2 == 0:
                 add_on("v", unit, 1)
+            if m >= 2:
+                quant(2 * m + 4)
+                quant(2 * m + 5)
             prev = unit if unit != v1 else prev
         finish(order[-1])

@@ -172,7 +172,7 @@ def tile_multiheadattention_pa_kernel(
             dst = grp[(hp, g)][:].rearrange("p (f e i t) -> p f e i t", f=2, e=2, i=64)
             src = (wide[(hp, g)] if hp < KP else wraw[(hp, g)][0])[:].rearrange("p t (e f i) -> p f e i t", e=2, f=2)
             if len(engs) == 1:
-                copy_on(engs, dst, src)
+                copy_on(engs, dst.rearrange("p f e i t -> p e f i t"), src.rearrange("p f e i t -> p e f i t"))
             else:
                 for half in range(2):
                     copy_on(engs[half], dst[:, half], src[:, half])
@@ -481,9 +481,9 @@ def tile_multiheadattention_pa_kernel(
             rope(unit, 0)
             rope(unit, 1)
             if m >= 1:
-                group(2 * m + 6, "pp")
-                group(2 * m + 7, "aa" if m % 4 == 0 else "pp")
-            if unit[0] < KP and m % 2 == 0:
+                group(2 * m + 6, "p")
+                group(2 * m + 7, "aa" if m % 4 == 0 else "p")
+            if unit[0] < KP and (m < 17):
                 add_on("v", unit, 1)
             if m >= 2:
                 quant(2 * m + 4)

@@ -482,7 +482,7 @@ def tile_multiheadattention_pa_kernel(
             rope(unit, 1)
             if m >= 1:
                 group(2 * m + 6, "p")
-                group(2 * m + 7, "aa" if m % 4 == 0 else "p")
+                group(2 * m + 7, "pa")
             if unit[0] < KP and (m < 17):
                 add_on("v", unit, 1)
             if m >= 2:

@@ -383,8 +383,8 @@ def tile_multiheadattention_pa_kernel(
 
         def first_prep(g):
             x_out(0, g, "aa")
-            w_group(KP, g, "vv")
-            w_group(VP, g, "vv")
+            w_group(KP, g, "v")
+            w_group(VP, g, "v")
             x_quant(0, g)
             w_quant(KP, g)
             w_quant(VP, g)
@@ -415,8 +415,8 @@ def tile_multiheadattention_pa_kernel(
         tab_gather(0, 1, "a")
         bias_turn()
         mx_pass((v0, k0), 3)
-        group(0, "vv")
-        group(1, "vv")
+        group(0, "v")
+        group(1, "v")
         quant(0)
         quant(1)
         rope(v0, 0)
@@ -425,8 +425,8 @@ def tile_multiheadattention_pa_kernel(
         x_out(1, 0, "aa")
         widen(4)
         widen(5)
-        group(2, "vv")
-        group(3, "vv")
+        group(2, "v")
+        group(3, "v")
         quant(2)
         quant(3)
         mx_all((0, 0))
@@ -440,8 +440,8 @@ def tile_multiheadattention_pa_kernel(
         rope(k0, 1)
         x_quant(1, 0)
         x_quant(1, 1)
-        group(4, "vv")
-        group(5, "vv")
+        group(4, "v")
+        group(5, "v")
         quant(4)
         quant(5)
 
@@ -455,8 +455,8 @@ def tile_multiheadattention_pa_kernel(
                 x_out(1, 2, "aa")
                 x_turn(1, 3)
                 x_out(1, 3, "aa")
-                group(6, "vv")
-                group(7, "vv")
+                group(6, "v")
+                group(7, "v")
                 quant(6)
                 quant(7)
             widen(2 * m + 8)
@@ -473,8 +473,8 @@ def tile_multiheadattention_pa_kernel(
                 x_quant(1, 2)
                 x_quant(1, 3)
             if m == 1:
-                tab_gather(1, 0, "p")
-                tab_gather(1, 1, "p")
+                tab_gather(1, 0, "v")
+                tab_gather(1, 1, "v")
             if m == 2:
                 tab_turn(1, 0, "v")
                 tab_turn(1, 1, "v")

@@ -12,21 +12,16 @@ FP8X4 = mybir.dt.float8_e4m3fn_x4
 ADD = mybir.AluOpType.add
 MULT = mybir.AluOpType.mult
 COPY = mybir.ActivationFunctionType.Copy
-IDENT = mybir.ActivationFunctionType.Identity
 
 FLOPS = 2 * 1024 * 2048 * 2560
 
-WCB = 5
-WIDEB = 6
-GRPB = 4
-UWB = 3
-OKVB = 1
-WBB = {2: 8, 4: 4}
 P = 128
 G = 4
 KP = 8
 VP = 9
 SECTIONS = ((0, 0, 16), (1, 16, 24), (2, 40, 24))
+WBB = {2: 8, 4: 4}
+GRPB = {"v": 3, "p": 1}
 
 
 def tile_multiheadattention_pa_kernel(
@@ -44,13 +39,13 @@ def tile_multiheadattention_pa_kernel(
         const = ctx.enter_context(tc.tile_pool(name="const", bufs=1))
         xr_pool = ctx.enter_context(tc.tile_pool(name="xr_pool", bufs=6))
         wb_pool = ctx.enter_context(tc.tile_pool(name="wb_pool", bufs=8))
-        kv_pool = ctx.enter_context(tc.tile_pool(name="kv_pool", bufs=8))
+        kv_pool = ctx.enter_context(tc.tile_pool(name="kv_pool", bufs=4))
         tb_pool = ctx.enter_context(tc.tile_pool(name="tb_pool", bufs=4))
-        wc_pool = ctx.enter_context(tc.tile_pool(name="wc_pool", bufs=WCB))
+        wc_pool = ctx.enter_context(tc.tile_pool(name="wc_pool", bufs=4))
         xg_pool = ctx.enter_context(tc.tile_pool(name="xg_pool", bufs=2))
-        wide_pool = ctx.enter_context(tc.tile_pool(name="wide_pool", bufs=WIDEB))
-        grp_pool = ctx.enter_context(tc.tile_pool(name="grp_pool", bufs=GRPB))
-        uw_pool = ctx.enter_context(tc.tile_pool(name="uw_pool", bufs=UWB))
+        wide_pool = ctx.enter_context(tc.tile_pool(name="wide_pool", bufs=6))
+        grp_pool = ctx.enter_context(tc.tile_pool(name="grp_pool", bufs=3))
+        uw_pool = ctx.enter_context(tc.tile_pool(name="uw_pool", bufs=6))
         o_pool = ctx.enter_context(tc.tile_pool(name="o_pool", bufs=3))
         acc_pool = ctx.enter_context(tc.psum_pool(name="acc_pool", bufs=4))
         tr_pool = ctx.enter_context(tc.psum_pool(name="tr_pool", bufs=4))
@@ -65,14 +60,21 @@ def tile_multiheadattention_pa_kernel(
         ident_f = const.tile([P, P], F32, name="ident_f")
         masks.make_identity(nc, ident_f[:])
         ident_b = const.tile([P, P], BF16, name="ident_b")
-        masks.make_identity(nc, ident_b[:])
+        nc.vector.tensor_copy(out=ident_b[:], in_=ident_f[:])
+        swap_f = const.tile([P, P], F32, name="swap_f")
+        for half in range(2):
+            nc.vector.tensor_copy(
+                out=swap_f[:, half * 64 : half * 64 + 64], in_=ident_f[:, 64 - half * 64 : 128 - half * 64]
+            )
 
         wsc = const.tile([P, 16], F32, name="wsc")
         mk_b = const.tile([P, 8], BF16, name="mk_b")
         mk = const.tile([P, 8], F32, name="mk")
         x_codes = const.tile([P, G, 2, 512], U32, name="x_codes", align_bytes=64)
         x_scales = const.tile([P, G, 2, 512], U8, name="x_scales", align_bytes=64)
-        tabT = const.tile([P, 4, 1024], BF16, name="tabT")
+        kv_codes = const.tile([P, G, 512], U32, name="kv_codes", align_bytes=64)
+        kv_scales = const.tile([P, G, 512], U8, name="kv_scales", align_bytes=64)
+        tabT = const.tile([P, 2, 1024], BF16, name="tabT")
         biasT = const.tile([P, 20], F32, name="biasT")
 
         def copy_on(eng, out, in_):
@@ -85,6 +87,7 @@ def tile_multiheadattention_pa_kernel(
 
         xr = {}
         wraw = {}
+        kvraw = {}
         traw = {}
 
         def load_x(j, g):
@@ -92,10 +95,9 @@ def tile_multiheadattention_pa_kernel(
             nc.sync.dma_start(out=xr[(j, g)][:], in_=x_v[j, g])
 
         def load_kv(g):
+            kvraw[g] = kv_pool.tile([P, 2, 4, 256], BF16, name="kvraw", tag="kvraw")
             for m in range(2):
-                kvraw = kv_pool.tile([P, 4, 256], BF16, name="kvraw", tag="kvraw")
-                nc.sync.dma_start(out=kvraw[:], in_=wkv_v[m][g])
-                wraw[(KP + m, g)] = (kvraw, 0)
+                nc.sync.dma_start(out=kvraw[g][:, m], in_=wkv_v[m][g])
 
         def load_wq(hp0, n, g):
             wq_sb = wb_pool.tile([P, 4, n * 256], U8, name="wq_sb%d" % n, tag="wq_sb%d" % n, bufs=WBB[n])
@@ -120,13 +122,9 @@ def tile_multiheadattention_pa_kernel(
                 in_=mask[0].rearrange("(j r b) -> r j b", j=2, r=P, b=4),
             )
 
-        def load_bias(half, eng):
-            for vec, row, n in ((bq, 0, 8), (bk, 8, 1), (bv, 9, 1)):
-                r0 = half * 10 + row
-                eng.dma_start(
-                    out=brow[r0 : r0 + n, :].rearrange("h (e i) -> h e i", e=2),
-                    in_=vec.rearrange("(h e f i) -> f h e i", e=2, f=2, i=64)[half],
-                )
+        def load_bias(eng):
+            for vec, row, n in ((bq, 0, 16), (bk, 16, 2), (bv, 18, 2)):
+                eng.dma_start(out=brow[row : row + n, :], in_=vec.rearrange("(h d) -> h d", d=P))
 
         xt = {}
         xg = {}
@@ -167,50 +165,61 @@ def tile_multiheadattention_pa_kernel(
                     scale=wsc[:, 4 * g + t : 4 * g + t + 1],
                 )
 
-        def w_group(hp, g, engs):
-            grp[(hp, g)] = grp_pool.tile([P, 1024], BF16, name="grp", tag="grp", align_bytes=64)
-            dst = grp[(hp, g)][:].rearrange("p (f e i t) -> p f e i t", f=2, e=2, i=64)
-            src = (wide[(hp, g)] if hp < KP else wraw[(hp, g)][0])[:].rearrange("p t (e f i) -> p f e i t", e=2, f=2)
-            if len(engs) == 1:
-                copy_on(engs, dst.rearrange("p f e i t -> p e f i t"), src.rearrange("p f e i t -> p e f i t"))
-            else:
-                for half in range(2):
-                    copy_on(engs[half], dst[:, half], src[:, half])
+        def w_group(hp, g, eng):
+            tag = "grp_" + eng
+            grp[(hp, g)] = grp_pool.tile([P, 256, 4], BF16, name=tag, tag=tag, bufs=GRPB[eng], align_bytes=64)
+            copy_on(eng, grp[(hp, g)][:], wide[(hp, g)][:].rearrange("p t n -> p n t"))
 
         def w_quant(hp, g):
             if g == 0:
                 codes = wc_pool.tile([P, G, 256], U32, name="w_codes", tag="w_codes", align_bytes=64)
                 scales = wc_pool.tile([P, G, 256], U8, name="w_scales", tag="w_scales", align_bytes=64)
-                wts[hp] = (codes, scales)
+                wts[hp] = (codes, scales, 0)
             nc.vector.quantize_mx(
-                out=wts[hp][0][:, g, :].bitcast(FP8X4), scales=wts[hp][1][:, g, :], in_=grp[(hp, g)][:]
+                out=wts[hp][0][:, g, :].bitcast(FP8X4),
+                scales=wts[hp][1][:, g, :],
+                in_=grp[(hp, g)][:].rearrange("p n t -> p (n t)"),
+            )
+
+        wts[KP] = (kv_codes, kv_scales, 0)
+        wts[VP] = (kv_codes, kv_scales, 256)
+
+        def kv_group(g):
+            grp[(KP, g)] = grp_pool.tile([P, 2, 256, 4], BF16, name="grp_kv", tag="grp_kv", bufs=2, align_bytes=64)
+            nc.vector.tensor_copy(out=grp[(KP, g)][:], in_=kvraw[g][:].rearrange("p m t n -> p m n t"))
+
+        def kv_quant(g):
+            nc.vector.quantize_mx(
+                out=kv_codes[:, g, :].bitcast(FP8X4),
+                scales=kv_scales[:, g, :],
+                in_=grp[(KP, g)][:].rearrange("p m n t -> p (m n t)"),
             )
 
         asm = {}
 
-        def tab_gather(j, a, eng):
-            asm[(j, a)] = tb_pool.tile([P, 4, 256], BF16, name="asm", tag="asm")
-            dst = asm[(j, a)][:].rearrange("p b (f d i) -> p b f d i", f=2, d=2)
-            src = traw[(j, a)][:].rearrange("p t (b f i) -> p t b f i", b=4, f=2)
+        def tab_gather(j, eng):
+            asm[j] = tb_pool.tile([P, 2, 4, P], BF16, name="asm", tag="asm", bufs=2)
+            dst = asm[j][:].rearrange("p a b (f i) -> p a b f i", f=2)
+            src = [traw[(j, a)][:].rearrange("p t (b f i) -> p t b f i", b=4, f=2) for a in range(2)]
             for tb, c0, n in SECTIONS:
-                for dup in range(2):
-                    copy_on(eng, dst[:, :, :, dup, c0 : c0 + n], src[:, tb, :, :, c0 : c0 + n])
-
-        def tab_turn(j, a, eng):
-            for half in range(2):
-                pt = tr_pool.tile([P, 4, P], BF16, name="pt", tag="tr")
-                for b in range(4):
-                    nc.tensor.transpose(
-                        out=pt[:, b, :], in_=asm[(j, a)][:, b, half * P : (half + 1) * P], identity=ident_b[:]
-                    )
-                sign = -1.0 if (a == 1 and half == 0) else 1.0
-                dst = tabT[:, 2 * a + half, j * 512 : (j + 1) * 512]
+                cs = slice(c0, c0 + n)
+                copy_on(eng, dst[:, 0, :, :, cs], src[0][:, tb, :, :, cs])
+                copy_on(eng, dst[:, 1, :, 0, cs], src[1][:, tb, :, 1, cs])
                 if eng == "a":
-                    nc.scalar.activation(out=dst, in_=pt[:].rearrange("p b r -> p (b r)"), func=COPY, scale=sign)
+                    nc.scalar.activation(out=dst[:, 1, :, 1, cs], in_=src[1][:, tb, :, 0, cs], func=COPY, scale=-1.0)
                 else:
                     nc.vector.tensor_scalar(
-                        out=dst, in0=pt[:].rearrange("p b r -> p (b r)"), scalar1=sign, scalar2=None, op0=MULT
+                        out=dst[:, 1, :, 1, cs], in0=src[1][:, tb, :, 0, cs], scalar1=-1.0, scalar2=None, op0=MULT
                     )
+
+        def tab_turn(j):
+            pt = tr_pool.tile([P, 2, 4, P], BF16, name="pt", tag="tr")
+            for a in range(2):
+                for b in range(4):
+                    nc.tensor.transpose(out=pt[:, a, b, :], in_=asm[j][:, a, b, :], identity=ident_b[:])
+            nc.vector.tensor_copy(
+                out=tabT[:, :, j * 512 : (j + 1) * 512], in_=pt[:].rearrange("p a b r -> p a (b r)")
+            )
 
         def bias_turn():
             pb = tr_pool.tile([P, P], BF16, name="pb", tag="tr")
@@ -220,86 +229,71 @@ def tile_multiheadattention_pa_kernel(
 
         accs = {}
         uw = {}
-        summed = set()
 
-        def mx(unit, half, g):
+        def mx(unit, e, g):
             hp, j = unit
             if g == 0:
-                accs[(unit, half)] = acc_pool.tile([P, 512], F32, name="acc", tag="acc")
-            cols = slice(half * P, (half + 1) * P)
+                accs[(unit, e)] = acc_pool.tile([P, 512], F32, name="acc", tag="acc")
+            codes, scales, c0 = wts[hp]
+            cols = slice(c0 + e * P, c0 + (e + 1) * P)
             nc.tensor.matmul_mx(
-                out=accs[(unit, half)][:],
-                lhsT=wts[hp][0][:, g, cols].bitcast(FP8X4),
-                lhsT_scale=wts[hp][1][:, g, cols],
+                out=accs[(unit, e)][:],
+                lhsT=codes[:, g, cols].bitcast(FP8X4),
+                lhsT_scale=scales[:, g, cols],
                 rhs=x_codes[:, g, j, :].bitcast(FP8X4),
                 rhs_scale=x_scales[:, g, j, :],
                 start=(g == 0),
                 stop=(g == G - 1),
             )
 
-        def rope(unit, half, eng="v"):
+        def rope(unit, e):
             hp, j = unit
-            bias = biasT[:, 10 * half + hp : 10 * half + hp + 1]
-            acc = accs[(unit, half)]
+            bias = biasT[:, 2 * hp + e : 2 * hp + e + 1]
+            acc = accs[(unit, e)]
             if hp == VP:
-                name = ("u_lo", "u_hi")[half]
-                uw[(unit, name)] = uw_pool.tile([P, 512], F32, name=name, tag=name)
-                if eng == "a":
-                    nc.scalar.activation(out=uw[(unit, name)][:], in_=acc[:], func=IDENT, bias=bias)
-                else:
-                    nc.vector.tensor_scalar(out=uw[(unit, name)][:], in0=acc[:], scalar1=bias, scalar2=None, op0=ADD)
+                uw[(unit, e)] = (uw_pool.tile([P, 512], F32, name="uw0", tag="uw0"),)
+                nc.vector.tensor_scalar(out=uw[(unit, e)][0][:], in0=acc[:], scalar1=bias, scalar2=None, op0=ADD)
                 return
-            for name, k in ((("u_lo", 0), ("w_hi", 3)), (("w_lo", 2), ("u_hi", 1)))[half]:
-                uw[(unit, name)] = uw_pool.tile([P, 512], F32, name=name, tag=name)
+            u = uw_pool.tile([P, 512], F32, name="uw0", tag="uw0")
+            w = uw_pool.tile([P, 512], F32, name="uw1", tag="uw1")
+            uw[(unit, e)] = (u, w)
+            for a in range(2):
                 nc.vector.scalar_tensor_tensor(
-                    out=uw[(unit, name)][:],
+                    out=uw[(unit, e)][a][:],
                     in0=acc[:],
                     scalar=bias,
-                    in1=tabT[:, k, j * 512 : (j + 1) * 512],
+                    in1=tabT[:, a, j * 512 : (j + 1) * 512],
                     op0=ADD,
                     op1=MULT,
                 )
 
-        def add_on(eng, unit, half):
-            u = uw[(unit, ("u_lo", "u_hi")[half])]
-            w = uw[(unit, ("w_lo", "w_hi")[half])]
-            summed.add((unit, half))
-            if eng == "v":
-                nc.vector.tensor_tensor(out=u[:], in0=u[:], in1=w[:], op=ADD)
-            else:
-                nc.gpsimd.tensor_tensor(out=u[:], in0=u[:], in1=w[:], op=ADD)
-
-        def turn_back(dst, unit, half, b):
-            u = uw[(unit, ("u_lo", "u_hi")[half])]
-            w = uw.get((unit, ("w_lo", "w_hi")[half]))
+        def turn_back(dst, unit, e, b):
+            parts = uw[(unit, e)]
             bs = slice(b * P, (b + 1) * P)
-            if w is None or (unit, half) in summed:
-                nc.tensor.transpose(out=dst, in_=u[:, bs], identity=ident_f[:])
+            if len(parts) == 1:
+                nc.tensor.transpose(out=dst, in_=parts[0][:, bs], identity=ident_f[:])
             else:
-                nc.tensor.matmul(out=dst, lhsT=u[:, bs], rhs=ident_f[:], is_transpose=True, start=True, stop=False)
-                nc.tensor.matmul(out=dst, lhsT=w[:, bs], rhs=ident_f[:], is_transpose=True, start=False, stop=True)
+                nc.tensor.matmul(out=dst, lhsT=parts[0][:, bs], rhs=ident_f[:], is_transpose=True, start=True, stop=False)
+                nc.tensor.matmul(out=dst, lhsT=parts[1][:, bs], rhs=swap_f[:], is_transpose=True, start=False, stop=True)
 
         ob = {}
         o_sb = {}
 
-        def back_turn(unit, half):
-            ob[(unit, half)] = tr_pool.tile([P, 4, P], F32, name="ob", tag="tr")
+        def back_turn(unit, e):
+            ob[(unit, e)] = tr_pool.tile([P, 4, P], F32, name="ob", tag="tr")
             for b in range(4):
-                turn_back(ob[(unit, half)][:, b, :], unit, half, b)
+                turn_back(ob[(unit, e)][:, b, :], unit, e, b)
 
-        def back_out(unit, half):
-            if half == 0:
-                o_sb[unit] = o_pool.tile([P, 2, 4, 2, 64], F32, name="o", tag="o")
-            nc.scalar.copy(
-                out=o_sb[unit][:, :, :, half, :].rearrange("p e b i -> p b e i"),
-                in_=ob[(unit, half)][:].rearrange("p b (e i) -> p b e i", e=2),
-            )
+        def back_out(unit, e):
+            if e == 0:
+                o_sb[unit] = o_pool.tile([P, 2, 4, P], F32, name="o", tag="o")
+            nc.scalar.copy(out=o_sb[unit][:, e], in_=ob[(unit, e)][:])
 
-        def back_store(unit):
+        def back_store(unit, heads):
             hp, j = unit
             nc.sync.dma_start(
-                out=out_v[0][j][:, 2 * hp : 2 * hp + 2, :],
-                in_=o_sb[unit][:].rearrange("p e b f i -> p e (b f i)"),
+                out=out_v[0][j][:, 2 * hp + heads.start : 2 * hp + heads.stop, :],
+                in_=o_sb[unit][:, heads].rearrange("p e b d -> p e (b d)"),
             )
 
         okv = {}
@@ -307,32 +301,32 @@ def tile_multiheadattention_pa_kernel(
         def kv_turn(j, b):
             ob[(j, b)] = tr_pool.tile([P, 2, 2, P], F32, name="obkv", tag="tr")
             for q in range(2):
-                for half in range(2):
-                    turn_back(ob[(j, b)][:, half, q, :], (KP + q, j), half, b)
+                for e in range(2):
+                    turn_back(ob[(j, b)][:, q, e, :], (KP + q, j), e, b)
 
         def kv_out(j, b):
             if b == 0:
-                okv[j] = o_pool.tile([P, 2, 2, 4, 2, 64], F32, name="okv", tag="okv", bufs=OKVB)
+                okv[j] = o_pool.tile([P, 2, 2, 4, P], F32, name="okv", tag="okv", bufs=1)
             nc.scalar.activation(
-                out=okv[j][:, :, :, b, :, :].rearrange("p k e f i -> p (k e) f i"),
-                in_=ob[(j, b)][:].rearrange("p f k (e i) -> p (k e) f i", e=2),
+                out=okv[j][:, :, :, b, :],
+                in_=ob[(j, b)][:],
                 func=COPY,
                 scale=mk[:, 4 * j + b : 4 * j + b + 1],
             )
 
         def kv_store(j):
             for q in range(2):
-                nc.sync.dma_start(out=out_v[1 + q][j], in_=okv[j][:, q].rearrange("p e b f i -> p e (b f i)"))
+                nc.sync.dma_start(out=out_v[1 + q][j], in_=okv[j][:, q].rearrange("p e b d -> p e (b d)"))
 
         def mx_pass(pair, g):
             for unit in pair:
-                for half in range(2):
-                    mx(unit, half, g)
+                for e in range(2):
+                    mx(unit, e, g)
 
         def mx_all(unit):
-            for half in range(2):
+            for e in range(2):
                 for g in range(G):
-                    mx(unit, half, g)
+                    mx(unit, e, g)
 
         def finish_kv(j):
             for b in range(4):
@@ -341,38 +335,36 @@ def tile_multiheadattention_pa_kernel(
             kv_store(j)
 
         def finish(unit):
-            for half in range(2):
-                back_turn(unit, half)
-                back_out(unit, half)
-            back_store(unit)
+            for e in range(2):
+                back_turn(unit, e)
+                back_out(unit, e)
+            back_store(unit, slice(0, 2))
 
         k0, v0, k1, v1 = (KP, 0), (VP, 0), (KP, 1), (VP, 1)
-        sl = [(hp, g) for hp in range(8) for g in range(G)]
 
         def widen(s):
             if s < 32:
-                w_widen(sl[s][0], sl[s][1])
+                w_widen(s // 4, s % 4)
 
-        def group(s, engs):
+        def group(s, eng):
             if s < 32:
-                w_group(sl[s][0], sl[s][1], engs)
+                w_group(s // 4, s % 4, eng)
 
         def quant(s):
             if s < 32:
-                w_quant(sl[s][0], sl[s][1])
+                w_quant(s // 4, s % 4)
 
         load_wsc(nc.gpsimd)
-        load_bias(0, nc.gpsimd)
-        load_bias(1, nc.gpsimd)
+        load_bias(nc.gpsimd)
         load_mask(nc.gpsimd)
         load_x(0, 0)
         load_kv(0)
         load_x(0, 1)
         load_kv(1)
         load_wq(0, 2, 0)
-        load_wq(0, 2, 1)
         load_x(0, 2)
         load_kv(2)
+        load_wq(0, 2, 1)
         load_x(0, 3)
         load_kv(3)
         load_wq(0, 2, 2)
@@ -383,110 +375,104 @@ def tile_multiheadattention_pa_kernel(
 
         def first_prep(g):
             x_out(0, g, "aa")
-            w_group(KP, g, "v")
-            w_group(VP, g, "v")
+            kv_group(g)
             x_quant(0, g)
-            w_quant(KP, g)
-            w_quant(VP, g)
+            kv_quant(g)
 
         x_turn(0, 0)
+        load_x(1, 2)
         first_prep(0)
         x_turn(0, 1)
-        load_x(1, 2)
-        first_prep(1)
-        widen(0)
-        widen(1)
-        mx_pass((v0, k0), 0)
-        x_turn(0, 2)
         load_x(1, 3)
         for g in range(G):
             load_wq(2, 2, g)
         load_tab(1)
         for g in range(G):
             load_wq(4, 4, g)
+        first_prep(1)
+        mx_pass((v0, k0), 0)
+        widen(0)
+        x_turn(0, 2)
         first_prep(2)
         mx_pass((v0, k0), 1)
+        widen(1)
+        group(0, "v")
         x_turn(0, 3)
         first_prep(3)
+        mx_pass((v0, k0), 2)
+        quant(0)
         widen(2)
         widen(3)
-        mx_pass((v0, k0), 2)
-        tab_gather(0, 0, "a")
-        tab_gather(0, 1, "a")
+        group(1, "v")
         bias_turn()
         mx_pass((v0, k0), 3)
-        group(0, "v")
-        group(1, "v")
-        quant(0)
+        tab_gather(0, "a")
         quant(1)
+        group(2, "v")
         rope(v0, 0)
         rope(v0, 1)
+        group(3, "v")
+        quant(2)
+        tab_turn(0)
+        quant(3)
         x_turn(1, 0)
         x_out(1, 0, "aa")
         widen(4)
         widen(5)
-        group(2, "v")
-        group(3, "v")
-        quant(2)
-        quant(3)
         mx_all((0, 0))
-        tab_turn(0, 0, "v")
-        tab_turn(0, 1, "v")
+        rope(k0, 0)
+        rope(k0, 1)
+        group(5, "p")
+        group(4, "v")
+        x_quant(1, 0)
         x_turn(1, 1)
         x_out(1, 1, "aa")
         widen(6)
         widen(7)
-        rope(k0, 0)
-        rope(k0, 1)
-        x_quant(1, 0)
-        x_quant(1, 1)
-        group(4, "v")
-        group(5, "v")
+        finish_kv(0)
+        rope((0, 0), 0)
+        rope((0, 0), 1)
+        group(6, "v")
         quant(4)
         quant(5)
+        group(7, "p")
+        x_quant(1, 1)
+        quant(6)
+        x_turn(1, 2)
+        x_out(1, 2, "aa")
+        x_turn(1, 3)
+        x_out(1, 3, "aa")
+        x_quant(1, 2)
+        x_quant(1, 3)
+        quant(7)
 
-        order = [(0, 0), (1, 0), v1, k1, (0, 1), (1, 1)] + [(hp, j) for hp in range(2, 8) for j in range(2)]
-        prev = None
-        for m, unit in enumerate(order):
-            if m > 0:
-                mx_all(unit)
-            if m == 0:
-                x_turn(1, 2)
-                x_out(1, 2, "aa")
-                x_turn(1, 3)
-                x_out(1, 3, "aa")
-                group(6, "v")
-                group(7, "v")
-                quant(6)
-                quant(7)
-            widen(2 * m + 8)
-            widen(2 * m + 9)
-            if m == 0:
-                finish_kv(0)
-            elif unit == k1:
+        order = [(1, 0), v1, k1, (0, 1), (1, 1)] + [(hp, j) for hp in range(2, 8) for j in range(2)]
+        prev = (0, 0)
+        for m, unit in enumerate(order, 1):
+            mx_all(unit)
+            widen(2 * m + 6)
+            widen(2 * m + 7)
+            if unit == k1:
                 pass
             elif prev == k1:
                 finish_kv(1)
             else:
                 finish(prev)
-            if m == 0:
-                x_quant(1, 2)
-                x_quant(1, 3)
             if m == 1:
-                tab_gather(1, 0, "v")
-                tab_gather(1, 1, "v")
+                tab_gather(1, "v")
             if m == 2:
-                tab_turn(1, 0, "v")
-                tab_turn(1, 1, "v")
+                tab_turn(1)
             rope(unit, 0)
             rope(unit, 1)
-            if m >= 1:
-                group(2 * m + 6, "p")
-                group(2 * m + 7, "pa")
-            if unit[0] < KP and (m < 17):
-                add_on("v", unit, 1)
             if m >= 2:
-                quant(2 * m + 4)
-                quant(2 * m + 5)
+                group(2 * m + 4, "v")
+            if m >= 3:
+                quant(2 * m + 2)
+                quant(2 * m + 3)
+            if m >= 2:
+                group(2 * m + 5, "p")
             prev = unit if unit != v1 else prev
-        finish(order[-1])
+        for e in range(2):
+            back_turn(prev, e)
+            back_out(prev, e)
+            back_store(prev, slice(e, e + 1))

@@ -12,6 +12,7 @@ FP8X4 = mybir.dt.float8_e4m3fn_x4
 ADD = mybir.AluOpType.add
 MULT = mybir.AluOpType.mult
 COPY = mybir.ActivationFunctionType.Copy
+IDENT = mybir.ActivationFunctionType.Identity
 
 FLOPS = 2 * 1024 * 2048 * 2560
 
@@ -21,7 +22,7 @@ KP = 8
 VP = 9
 SECTIONS = ((0, 0, 16), (1, 16, 24), (2, 40, 24))
 WBB = {2: 8, 4: 4}
-GRPB = {"v": 3, "p": 1}
+GRPB = {"v": 3, "p": 1, "a": 2}
 
 
 def tile_multiheadattention_pa_kernel(
@@ -75,6 +76,8 @@ def tile_multiheadattention_pa_kernel(
         kv_codes = const.tile([P, G, 512], U32, name="kv_codes", align_bytes=64)
         kv_scales = const.tile([P, G, 512], U8, name="kv_scales", align_bytes=64)
         tabT = const.tile([P, 2, 1024], BF16, name="tabT")
+        bv_b = const.tile([P, 256], BF16, name="bv_b")
+        bv_m = const.tile([P, 4, 256], F32, name="bv_m")
         biasT = const.tile([P, 20], F32, name="biasT")
 
         def copy_on(eng, out, in_):
@@ -184,9 +187,13 @@ def tile_multiheadattention_pa_kernel(
         wts[KP] = (kv_codes, kv_scales, 0)
         wts[VP] = (kv_codes, kv_scales, 256)
 
-        def kv_group(g):
+        def kv_group(g, engs):
             grp[(KP, g)] = grp_pool.tile([P, 2, 256, 4], BF16, name="grp_kv", tag="grp_kv", bufs=2, align_bytes=64)
-            nc.vector.tensor_copy(out=grp[(KP, g)][:], in_=kvraw[g][:].rearrange("p m t n -> p m n t"))
+            if len(engs) == 1:
+                copy_on(engs, grp[(KP, g)][:], kvraw[g][:].rearrange("p m t n -> p m n t"))
+            else:
+                for m in range(2):
+                    copy_on(engs[m], grp[(KP, g)][:, m], kvraw[g][:, m].rearrange("p t n -> p n t"))
 
         def kv_quant(g):
             nc.vector.quantize_mx(
@@ -207,9 +214,13 @@ def tile_multiheadattention_pa_kernel(
                 copy_on(eng, dst[:, 1, :, 0, cs], src[1][:, tb, :, 1, cs])
                 if eng == "a":
                     nc.scalar.activation(out=dst[:, 1, :, 1, cs], in_=src[1][:, tb, :, 0, cs], func=COPY, scale=-1.0)
-                else:
+                elif eng == "v":
                     nc.vector.tensor_scalar(
                         out=dst[:, 1, :, 1, cs], in0=src[1][:, tb, :, 0, cs], scalar1=-1.0, scalar2=None, op0=MULT
+                    )
+                else:
+                    nc.gpsimd.tensor_scalar(
+                        out=dst[:, 1, :, 1, cs], in0=src[1][:, tb, :, 0, cs], scalar1=-1.0, scalar2=0.0, op0=MULT, op1=ADD
                     )
 
         def tab_turn(j):
@@ -217,9 +228,7 @@ def tile_multiheadattention_pa_kernel(
             for a in range(2):
                 for b in range(4):
                     nc.tensor.transpose(out=pt[:, a, b, :], in_=asm[j][:, a, b, :], identity=ident_b[:])
-            nc.vector.tensor_copy(
-                out=tabT[:, :, j * 512 : (j + 1) * 512], in_=pt[:].rearrange("p a b r -> p a (b r)")
-            )
+            nc.scalar.copy(out=tabT[:, :, j * 512 : (j + 1) * 512], in_=pt[:].rearrange("p a b r -> p a (b r)"))
 
         def bias_turn():
             pb = tr_pool.tile([P, P], BF16, name="pb", tag="tr")
@@ -252,7 +261,7 @@ def tile_multiheadattention_pa_kernel(
             acc = accs[(unit, e)]
             if hp == VP:
                 uw[(unit, e)] = (uw_pool.tile([P, 512], F32, name="uw0", tag="uw0"),)
-                nc.vector.tensor_scalar(out=uw[(unit, e)][0][:], in0=acc[:], scalar1=bias, scalar2=None, op0=ADD)
+                nc.scalar.activation(out=uw[(unit, e)][0][:], in_=acc[:], func=IDENT, bias=bias)
                 return
             u = uw_pool.tile([P, 512], F32, name="uw0", tag="uw0")
             w = uw_pool.tile([P, 512], F32, name="uw1", tag="uw1")
@@ -297,6 +306,63 @@ def tile_multiheadattention_pa_kernel(
             )
 
         okv = {}
+
+        def load_bv(eng):
+            eng.dma_start(out=bv_b[:], in_=bv.partition_broadcast(P))
+
+        def v_bias(j):
+            for b in range(4):
+                nc.gpsimd.tensor_scalar(
+                    out=bv_m[:, b, :], in0=bv_b[:], scalar1=mk[:, 4 * j + b : 4 * j + b + 1], scalar2=0.0, op0=MULT, op1=ADD
+                )
+
+        def v_mx(j):
+            for q in range(2):
+                acc = acc_pool.tile([P, 2, 256], F32, name="acc", tag="acc")
+                accs[("v", j, q)] = acc
+                for b2 in range(2):
+                    rows = slice((2 * q + b2) * P, (2 * q + b2 + 1) * P)
+                    for g in range(G):
+                        nc.tensor.matmul_mx(
+                            out=acc[:, b2, :],
+                            lhsT=x_codes[:, g, j, rows].bitcast(FP8X4),
+                            lhsT_scale=x_scales[:, g, j, rows],
+                            rhs=kv_codes[:, g, 256:512].bitcast(FP8X4),
+                            rhs_scale=kv_scales[:, g, 256:512],
+                            start=(g == 0),
+                            stop=(g == G - 1),
+                        )
+
+        def v_out(j):
+            okv[(VP, j)] = o_pool.tile([P, 2, 4, P], F32, name="o", tag="o")
+            for b in range(4):
+                nc.vector.scalar_tensor_tensor(
+                    out=okv[(VP, j)][:, :, b, :],
+                    in0=accs[("v", j, b // 2)][:, b % 2, :].rearrange("p (e d) -> p e d", e=2),
+                    scalar=mk[:, 4 * j + b : 4 * j + b + 1],
+                    in1=bv_m[:, b, :].rearrange("p (e d) -> p e d", e=2),
+                    op0=MULT,
+                    op1=ADD,
+                )
+            nc.sync.dma_start(out=out_v[2][j], in_=okv[(VP, j)][:].rearrange("p e b d -> p e (b d)"))
+
+        def k_turn(j):
+            for bb in range(2):
+                ob[(j, bb)] = tr_pool.tile([P, 2, 2, P], F32, name="obk", tag="tr")
+                for b2 in range(2):
+                    for e in range(2):
+                        turn_back(ob[(j, bb)][:, b2, e, :], (KP, j), e, 2 * bb + b2)
+
+        def k_out(j):
+            okv[(KP, j)] = o_pool.tile([P, 2, 4, P], F32, name="o", tag="o")
+            for b in range(4):
+                nc.scalar.activation(
+                    out=okv[(KP, j)][:, :, b, :],
+                    in_=ob[(j, b // 2)][:, b % 2],
+                    func=COPY,
+                    scale=mk[:, 4 * j + b : 4 * j + b + 1],
+                )
+            nc.sync.dma_start(out=out_v[1][j], in_=okv[(KP, j)][:].rearrange("p e b d -> p e (b d)"))
 
         def kv_turn(j, b):
             ob[(j, b)] = tr_pool.tile([P, 2, 2, P], F32, name="obkv", tag="tr")
@@ -354,9 +420,9 @@ def tile_multiheadattention_pa_kernel(
             if s < 32:
                 w_quant(s // 4, s % 4)
 
-        load_wsc(nc.gpsimd)
-        load_bias(nc.gpsimd)
-        load_mask(nc.gpsimd)
+        load_wsc(nc.scalar)
+        load_mask(nc.scalar)
+        load_bias(nc.scalar)
         load_x(0, 0)
         load_kv(0)
         load_x(0, 1)
@@ -367,15 +433,16 @@ def tile_multiheadattention_pa_kernel(
         load_wq(0, 2, 1)
         load_x(0, 3)
         load_kv(3)
+        load_tab(0)
+        load_bv(nc.sync)
         load_wq(0, 2, 2)
         load_wq(0, 2, 3)
-        load_tab(0)
         load_x(1, 0)
         load_x(1, 1)
 
         def first_prep(g):
             x_out(0, g, "aa")
-            kv_group(g)
+            kv_group(g, "v")
             x_quant(0, g)
             kv_quant(g)
 
@@ -384,9 +451,9 @@ def tile_multiheadattention_pa_kernel(
         first_prep(0)
         x_turn(0, 1)
         load_x(1, 3)
+        load_tab(1)
         for g in range(G):
             load_wq(2, 2, g)
-        load_tab(1)
         for g in range(G):
             load_wq(4, 4, g)
         first_prep(1)
@@ -400,79 +467,82 @@ def tile_multiheadattention_pa_kernel(
         x_turn(0, 3)
         first_prep(3)
         mx_pass((v0, k0), 2)
+        widen(4)
         quant(0)
+        tab_gather(0, "v")
         widen(2)
-        widen(3)
         group(1, "v")
         bias_turn()
         mx_pass((v0, k0), 3)
-        tab_gather(0, "a")
-        quant(1)
-        group(2, "v")
+        widen(3)
         rope(v0, 0)
         rope(v0, 1)
+        tab_turn(0)
+        quant(1)
+        group(2, "v")
         group(3, "v")
         quant(2)
-        tab_turn(0)
-        quant(3)
         x_turn(1, 0)
         x_out(1, 0, "aa")
-        widen(4)
-        widen(5)
+        quant(3)
         mx_all((0, 0))
+        widen(5)
         rope(k0, 0)
         rope(k0, 1)
-        group(5, "p")
         group(4, "v")
-        x_quant(1, 0)
         x_turn(1, 1)
         x_out(1, 1, "aa")
-        widen(6)
-        widen(7)
+        x_quant(1, 0)
+        quant(4)
+        x_quant(1, 1)
+        group(5, "p")
+        v_bias(1)
         finish_kv(0)
         rope((0, 0), 0)
         rope((0, 0), 1)
-        group(6, "v")
-        quant(4)
-        quant(5)
-        group(7, "p")
-        x_quant(1, 1)
-        quant(6)
         x_turn(1, 2)
         x_out(1, 2, "aa")
         x_turn(1, 3)
         x_out(1, 3, "aa")
         x_quant(1, 2)
         x_quant(1, 3)
-        quant(7)
+        tab_gather(1, "v")
+        quant(5)
+        widen(6)
+        widen(7)
+        group(6, "v")
+        group(7, "p")
 
-        order = [(1, 0), v1, k1, (0, 1), (1, 1)] + [(hp, j) for hp in range(2, 8) for j in range(2)]
+        units = [v1, k1] + [(hp, j) for hp in range(8) for j in range(2)][1:]
         prev = (0, 0)
-        for m, unit in enumerate(order, 1):
-            mx_all(unit)
+        for m, unit in enumerate(units, 1):
+            if m == 1:
+                v_mx(1)
+                tab_turn(1)
+                v_out(1)
+            elif m == 2:
+                mx_all(k1)
+            elif m % 2 == 1:
+                mx_all(unit)
+                if m < 17:
+                    mx_all(units[m])
             widen(2 * m + 6)
             widen(2 * m + 7)
-            if unit == k1:
-                pass
-            elif prev == k1:
-                finish_kv(1)
-            else:
-                finish(prev)
-            if m == 1:
-                tab_gather(1, "v")
             if m == 2:
-                tab_turn(1)
-            rope(unit, 0)
-            rope(unit, 1)
-            if m >= 2:
-                group(2 * m + 4, "v")
-            if m >= 3:
-                quant(2 * m + 2)
-                quant(2 * m + 3)
-            if m >= 2:
-                group(2 * m + 5, "p")
-            prev = unit if unit != v1 else prev
+                finish((0, 0))
+            elif m == 3:
+                k_turn(1)
+                k_out(1)
+            elif m > 3:
+                finish(units[m - 2])
+            if m > 1:
+                rope(unit, 0)
+                rope(unit, 1)
+            group(2 * m + 6, "v")
+            quant(2 * m + 4)
+            quant(2 * m + 5)
+            group(2 * m + 7, "p")
         for e in range(2):
-            back_turn(prev, e)
-            back_out(prev, e)
-            back_store(prev, slice(e, e + 1))
+            back_turn((7, 1), e)
+            back_out((7, 1), e)
+            back_store((7, 1), slice(e, e + 1))

@@ -94,23 +94,23 @@ def tile_multiheadattention_pa_kernel(
         traw = {}
 
         def load_x(j, g):
-            xr[(j, g)] = xr_pool.tile([P, 4, 512], BF16, name="xr", tag="xr")
+            xr[(j, g)] = xr_pool.tile([P, 4, 512], BF16, name="xr", tag="xr", align_bytes=256)
             nc.sync.dma_start(out=xr[(j, g)][:], in_=x_v[j, g])
 
         def load_kv(g):
-            kvraw[g] = kv_pool.tile([P, 2, 4, 256], BF16, name="kvraw", tag="kvraw")
+            kvraw[g] = kv_pool.tile([P, 2, 4, 256], BF16, name="kvraw", tag="kvraw", align_bytes=256)
             for m in range(2):
                 nc.sync.dma_start(out=kvraw[g][:, m], in_=wkv_v[m][g])
 
         def load_wq(hp0, n, g):
-            wq_sb = wb_pool.tile([P, 4, n * 256], U8, name="wq_sb%d" % n, tag="wq_sb%d" % n, bufs=WBB[n])
+            wq_sb = wb_pool.tile([P, 4, n * 256], U8, name="wq_sb%d" % n, tag="wq_sb%d" % n, bufs=WBB[n], align_bytes=256)
             nc.sync.dma_start(out=wq_sb[:], in_=wq_v[g][:, :, hp0 * 256 : (hp0 + n) * 256])
             for i in range(n):
                 wraw[(hp0 + i, g)] = (wq_sb, i)
 
         def load_tab(j):
             for a in range(2):
-                traw[(j, a)] = tb_pool.tile([P, 3, 512], BF16, name="traw", tag="traw")
+                traw[(j, a)] = tb_pool.tile([P, 3, 512], BF16, name="traw", tag="traw", align_bytes=256)
                 nc.sync.dma_start(out=traw[(j, a)][:], in_=tab_v[a][j])
 
         def load_wsc(eng):
@@ -171,7 +171,13 @@ def tile_multiheadattention_pa_kernel(
         def w_group(hp, g, eng):
             tag = "grp_" + eng
             grp[(hp, g)] = grp_pool.tile([P, 256, 4], BF16, name=tag, tag=tag, bufs=GRPB[eng], align_bytes=64)
-            copy_on(eng, grp[(hp, g)][:], wide[(hp, g)][:].rearrange("p t n -> p n t"))
+            if eng == "v":
+                nc.vector.tensor_copy(
+                    out=grp[(hp, g)][:].rearrange("p (c i) t -> p c t i", i=4),
+                    in_=wide[(hp, g)][:].rearrange("p t (c i) -> p c t i", i=4),
+                )
+            else:
+                copy_on(eng, grp[(hp, g)][:], wide[(hp, g)][:].rearrange("p t n -> p n t"))
 
         def w_quant(hp, g):
             if g == 0:
@@ -190,7 +196,11 @@ def tile_multiheadattention_pa_kernel(
         def kv_group(g, engs):
             grp[(KP, g)] = grp_pool.tile([P, 2, 256, 4], BF16, name="grp_kv", tag="grp_kv", bufs=2, align_bytes=64)
             if len(engs) == 1:
-                copy_on(engs, grp[(KP, g)][:], kvraw[g][:].rearrange("p m t n -> p m n t"))
+                for m in range(2):
+                    nc.vector.tensor_copy(
+                        out=grp[(KP, g)][:, m].rearrange("p (c i) t -> p c t i", i=4),
+                        in_=kvraw[g][:, m].rearrange("p t (c i) -> p c t i", i=4),
+                    )
             else:
                 for m in range(2):
                     copy_on(engs[m], grp[(KP, g)][:, m], kvraw[g][:, m].rearrange("p t n -> p n t"))
@@ -295,7 +305,7 @@ def tile_multiheadattention_pa_kernel(
 
         def back_out(unit, e):
             if e == 0:
-                o_sb[unit] = o_pool.tile([P, 2, 4, P], F32, name="o", tag="o")
+                o_sb[unit] = o_pool.tile([P, 2, 4, P], F32, name="o", tag="o", align_bytes=256)
             nc.scalar.copy(out=o_sb[unit][:, e], in_=ob[(unit, e)][:])
 
         def back_store(unit, heads):
@@ -334,7 +344,7 @@ def tile_multiheadattention_pa_kernel(
                         )
 
         def v_out(j):
-            okv[(VP, j)] = o_pool.tile([P, 2, 4, P], F32, name="o", tag="o")
+            okv[(VP, j)] = o_pool.tile([P, 2, 4, P], F32, name="o", tag="o", align_bytes=256)
             for b in range(4):
                 nc.vector.scalar_tensor_tensor(
                     out=okv[(VP, j)][:, :, b, :],
@@ -354,7 +364,7 @@ def tile_multiheadattention_pa_kernel(
                         turn_back(ob[(j, bb)][:, b2, e, :], (KP, j), e, 2 * bb + b2)
 
         def k_out(j):
-            okv[(KP, j)] = o_pool.tile([P, 2, 4, P], F32, name="o", tag="o")
+            okv[(KP, j)] = o_pool.tile([P, 2, 4, P], F32, name="o", tag="o", align_bytes=256)
             for b in range(4):
                 nc.scalar.activation(
                     out=okv[(KP, j)][:, :, b, :],
@@ -372,7 +382,7 @@ def tile_multiheadattention_pa_kernel(
 
         def kv_out(j, b):
             if b == 0:
-                okv[j] = o_pool.tile([P, 2, 2, 4, P], F32, name="okv", tag="okv", bufs=1)
+                okv[j] = o_pool.tile([P, 2, 2, 4, P], F32, name="okv", tag="okv", bufs=1, align_bytes=256)
             nc.scalar.activation(
                 out=okv[j][:, :, :, b, :],
                 in_=ob[(j, b)][:],

@@ -54,8 +54,6 @@ def tile_multiheadattention_pa_kernel(
 
         zero1 = const.tile([P, 1], F32, name="zero1")
         nc.vector.memset(zero1[:], 0.0)
-        warm = const.tile([P, 1], F32, name="warm")
-        nc.scalar.activation(out=warm[:], in_=zero1[:], func=COPY)
         brow = const.tile([P, P], BF16, name="brow")
         nc.vector.memset(brow[:], 0.0)
         ident_f = const.tile([P, P], F32, name="ident_f")
@@ -77,8 +75,21 @@ def tile_multiheadattention_pa_kernel(
         kv_scales = const.tile([P, G, 512], U8, name="kv_scales", align_bytes=64)
         tabT = const.tile([P, 2, 1024], BF16, name="tabT")
         bv_b = const.tile([P, 256], BF16, name="bv_b")
+        bq_b = const.tile([P, 256], BF16, name="bq_b")
         bv_m = const.tile([P, 4, 256], F32, name="bv_m")
         biasT = const.tile([P, 20], F32, name="biasT")
+
+        nc.scalar.dma_start(
+            out=wsc[:].rearrange("p (g t) -> p g t", t=4),
+            in_=Wq_scale.rearrange("(g p t) o -> p g (t o)", g=G, p=P, t=4),
+        )
+        for vec, row, n in ((bq, 0, 16), (bk, 16, 2), (bv, 18, 2)):
+            nc.scalar.dma_start(out=brow[row : row + n, :], in_=vec.rearrange("(h d) -> h d", d=P))
+        nc.scalar.dma_start(
+            out=mk_b[:].rearrange("p (j b) -> p j b", b=4), in_=mask[0].rearrange("(j r b) -> r j b", j=2, r=P, b=4)
+        )
+        warm = const.tile([P, 1], F32, name="warm")
+        nc.scalar.activation(out=warm[:], in_=zero1[:], func=COPY)
 
         def copy_on(eng, out, in_):
             if eng == "v":
@@ -113,22 +124,6 @@ def tile_multiheadattention_pa_kernel(
                 traw[(j, a)] = tb_pool.tile([P, 3, 512], BF16, name="traw", tag="traw", align_bytes=256)
                 nc.sync.dma_start(out=traw[(j, a)][:], in_=tab_v[a][j])
 
-        def load_wsc(eng):
-            eng.dma_start(
-                out=wsc[:].rearrange("p (g t) -> p g t", t=4),
-                in_=Wq_scale.rearrange("(g p t) o -> p g (t o)", g=G, p=P, t=4),
-            )
-
-        def load_mask(eng):
-            eng.dma_start(
-                out=mk_b[:].rearrange("p (j b) -> p j b", b=4),
-                in_=mask[0].rearrange("(j r b) -> r j b", j=2, r=P, b=4),
-            )
-
-        def load_bias(eng):
-            for vec, row, n in ((bq, 0, 16), (bk, 16, 2), (bv, 18, 2)):
-                eng.dma_start(out=brow[row : row + n, :], in_=vec.rearrange("(h d) -> h d", d=P))
-
         xt = {}
         xg = {}
 
@@ -157,16 +152,17 @@ def tile_multiheadattention_pa_kernel(
         grp = {}
         wts = {}
 
-        def w_widen(hp, g):
+        def w_widen(hp, g, on_vector=0):
             wide[(hp, g)] = wide_pool.tile([P, 4, 256], BF16, name="wide", tag="wide")
             raw, i = wraw[(hp, g)]
             for t in range(4):
-                nc.scalar.activation(
-                    out=wide[(hp, g)][:, t, :],
-                    in_=raw[:, t, i * 256 : (i + 1) * 256].bitcast(FP8),
-                    func=COPY,
-                    scale=wsc[:, 4 * g + t : 4 * g + t + 1],
-                )
+                out = wide[(hp, g)][:, t, :]
+                in_ = raw[:, t, i * 256 : (i + 1) * 256].bitcast(FP8)
+                scale = wsc[:, 4 * g + t : 4 * g + t + 1]
+                if t < 4 - on_vector:
+                    nc.scalar.activation(out=out, in_=in_, func=COPY, scale=scale)
+                else:
+                    nc.vector.tensor_scalar(out=out, in0=in_, scalar1=scale, scalar2=None, op0=MULT)
 
         def w_group(hp, g, eng):
             tag = "grp_" + eng
@@ -248,6 +244,8 @@ def tile_multiheadattention_pa_kernel(
 
         accs = {}
         uw = {}
+        ob = {}
+        o_sb = {}
 
         def mx(unit, e, g):
             hp, j = unit
@@ -295,8 +293,6 @@ def tile_multiheadattention_pa_kernel(
                 nc.tensor.matmul(out=dst, lhsT=parts[0][:, bs], rhs=ident_f[:], is_transpose=True, start=True, stop=False)
                 nc.tensor.matmul(out=dst, lhsT=parts[1][:, bs], rhs=swap_f[:], is_transpose=True, start=False, stop=True)
 
-        ob = {}
-        o_sb = {}
 
         def back_turn(unit, e):
             ob[(unit, e)] = tr_pool.tile([P, 4, P], F32, name="ob", tag="tr")
@@ -355,6 +351,73 @@ def tile_multiheadattention_pa_kernel(
                     op1=ADD,
                 )
             nc.sync.dma_start(out=out_v[2][j], in_=okv[(VP, j)][:].rearrange("p e b d -> p e (b d)"))
+
+        def load_bq_last(eng):
+            eng.dma_start(out=bq_b[:], in_=bq[14 * P : 16 * P].partition_broadcast(P))
+
+        def xs_mx(unit):
+            hp, j = unit
+            codes, scales, c0 = wts[hp]
+            for q in range(2):
+                acc = acc_pool.tile([P, 2, 256], F32, name="acc", tag="acc")
+                accs[(unit, q)] = acc
+                for b2 in range(2):
+                    rows = slice((2 * q + b2) * P, (2 * q + b2 + 1) * P)
+                    for g in range(G):
+                        nc.tensor.matmul_mx(
+                            out=acc[:, b2, :],
+                            lhsT=x_codes[:, g, j, rows].bitcast(FP8X4),
+                            lhsT_scale=x_scales[:, g, j, rows],
+                            rhs=codes[:, g, :].bitcast(FP8X4),
+                            rhs_scale=scales[:, g, :],
+                            start=(g == 0),
+                            stop=(g == G - 1),
+                        )
+
+        def xs_rope(unit, store=True):
+            hp, j = unit
+            o_sb[unit] = o_pool.tile([P, 2, 4, P], F32, name="o", tag="o", align_bytes=256)
+            t, u, w = {}, {}, {}
+            for q in range(2):
+                t[q] = uw_pool.tile([P, 2, 256], F32, name="uw0", tag="uw0")
+                nc.vector.tensor_tensor(
+                    out=t[q][:], in0=accs[(unit, q)][:], in1=bq_b[:].unsqueeze(1).to_broadcast([P, 2, 256]), op=ADD
+                )
+            for q in range(2):
+                u[q] = uw_pool.tile([P, 2, 2, P], F32, name="uw0", tag="uw0")
+                w[q] = uw_pool.tile([P, 2, 2, P], F32, name="uw1", tag="uw1")
+                for a, dst in ((0, u[q]), (1, w[q])):
+                    nc.vector.tensor_tensor(
+                        out=dst[:],
+                        in0=t[q][:].rearrange("p b (e d) -> p b e d", e=2),
+                        in1=asm[j][:, a, 2 * q : 2 * q + 2, :].unsqueeze(2).to_broadcast([P, 2, 2, P]),
+                        op=MULT,
+                    )
+            for q in range(2):
+                for half in range(2):
+                    lo, hi = 64 * half, 64 - 64 * half
+                    nc.vector.tensor_tensor(
+                        out=o_sb[unit][:, :, 2 * q : 2 * q + 2, lo : lo + 64],
+                        in0=u[q][:, :, :, lo : lo + 64].rearrange("p b e i -> p e b i"),
+                        in1=w[q][:, :, :, hi : hi + 64].rearrange("p b e i -> p e b i"),
+                        op=ADD,
+                    )
+            back_store(unit, slice(0, 2))
+
+        def last_finish(unit):
+            hp, j = unit
+            back_turn(unit, 0)
+            back_out(unit, 0)
+            back_store(unit, slice(0, 1))
+            for bb, copy in ((0, nc.scalar.copy), (1, nc.vector.tensor_copy)):
+                t = tr_pool.tile([P, 2, P], F32, name="ob", tag="tr")
+                for b2 in range(2):
+                    turn_back(t[:, b2, :], unit, 1, 2 * bb + b2)
+                copy(out=o_sb[unit][:, 1, 2 * bb : 2 * bb + 2, :], in_=t[:])
+                nc.sync.dma_start(
+                    out=out_v[0][j][:, 2 * hp + 1, 256 * bb : 256 * (bb + 1)],
+                    in_=o_sb[unit][:, 1, 2 * bb : 2 * bb + 2, :].rearrange("p b d -> p (b d)"),
+                )
 
         def k_turn(j):
             for bb in range(2):
@@ -418,9 +481,9 @@ def tile_multiheadattention_pa_kernel(
 
         k0, v0, k1, v1 = (KP, 0), (VP, 0), (KP, 1), (VP, 1)
 
-        def widen(s):
+        def widen(s, on_vector=0):
             if s < 32:
-                w_widen(s // 4, s % 4)
+                w_widen(s // 4, s % 4, on_vector)
 
         def group(s, eng):
             if s < 32:
@@ -430,35 +493,31 @@ def tile_multiheadattention_pa_kernel(
             if s < 32:
                 w_quant(s // 4, s % 4)
 
-        load_wsc(nc.scalar)
-        load_mask(nc.scalar)
-        load_bias(nc.scalar)
-        load_x(0, 0)
         load_kv(0)
-        load_x(0, 1)
+        load_x(0, 0)
         load_kv(1)
-        load_wq(0, 2, 0)
-        load_x(0, 2)
+        load_x(0, 1)
         load_kv(2)
-        load_wq(0, 2, 1)
-        load_x(0, 3)
+        load_x(0, 2)
         load_kv(3)
+        load_x(0, 3)
+        load_wq(0, 2, 0)
+        load_wq(0, 2, 1)
         load_tab(0)
         load_bv(nc.sync)
+        load_bq_last(nc.sync)
         load_wq(0, 2, 2)
         load_wq(0, 2, 3)
         load_x(1, 0)
         load_x(1, 1)
 
-        def first_prep(g):
-            x_out(0, g, "aa")
-            kv_group(g, "v")
-            x_quant(0, g)
-            kv_quant(g)
-
+        kv_group(0, "v")
         x_turn(0, 0)
         load_x(1, 2)
-        first_prep(0)
+        kv_quant(0)
+        x_out(0, 0, "aa")
+        kv_group(1, "v")
+        x_quant(0, 0)
         x_turn(0, 1)
         load_x(1, 3)
         load_tab(1)
@@ -466,29 +525,36 @@ def tile_multiheadattention_pa_kernel(
             load_wq(2, 2, g)
         for g in range(G):
             load_wq(4, 4, g)
-        first_prep(1)
+        kv_quant(1)
+        x_out(0, 1, "aa")
         mx_pass((v0, k0), 0)
-        widen(0)
+        kv_group(2, "v")
+        x_quant(0, 1)
         x_turn(0, 2)
-        first_prep(2)
+        x_out(0, 2, "aa")
         mx_pass((v0, k0), 1)
-        widen(1)
-        group(0, "v")
+        kv_quant(2)
+        kv_group(3, "v")
+        x_quant(0, 2)
         x_turn(0, 3)
-        first_prep(3)
+        x_out(0, 3, "aa")
+        widen(0)
+        kv_quant(3)
+        widen(1)
         mx_pass((v0, k0), 2)
-        widen(4)
-        quant(0)
-        tab_gather(0, "v")
+        x_quant(0, 3)
+        group(0, "v")
         widen(2)
         group(1, "v")
+        quant(0)
+        tab_gather(0, "v")
+        quant(1)
         bias_turn()
         mx_pass((v0, k0), 3)
         widen(3)
         rope(v0, 0)
         rope(v0, 1)
         tab_turn(0)
-        quant(1)
         group(2, "v")
         group(3, "v")
         quant(2)
@@ -496,35 +562,35 @@ def tile_multiheadattention_pa_kernel(
         x_out(1, 0, "aa")
         quant(3)
         mx_all((0, 0))
-        widen(5)
+        widen(4)
         rope(k0, 0)
         rope(k0, 1)
-        group(4, "v")
         x_turn(1, 1)
         x_out(1, 1, "aa")
         x_quant(1, 0)
-        quant(4)
-        x_quant(1, 1)
-        group(5, "p")
-        v_bias(1)
-        finish_kv(0)
-        rope((0, 0), 0)
-        rope((0, 0), 1)
         x_turn(1, 2)
         x_out(1, 2, "aa")
+        x_quant(1, 1)
+        v_bias(1)
+        rope((0, 0), 0)
+        rope((0, 0), 1)
         x_turn(1, 3)
         x_out(1, 3, "aa")
         x_quant(1, 2)
+        finish_kv(0)
         x_quant(1, 3)
         tab_gather(1, "v")
-        quant(5)
+        widen(5)
         widen(6)
+        group(4, "v")
+        group(5, "p")
         widen(7)
         group(6, "v")
+        quant(4)
+        quant(5)
         group(7, "p")
 
         units = [v1, k1] + [(hp, j) for hp in range(8) for j in range(2)][1:]
-        prev = (0, 0)
         for m, unit in enumerate(units, 1):
             if m == 1:
                 v_mx(1)
@@ -534,8 +600,10 @@ def tile_multiheadattention_pa_kernel(
                 mx_all(k1)
             elif m % 2 == 1:
                 mx_all(unit)
-                if m < 17:
+                if m < 15:
                     mx_all(units[m])
+                elif m == 15:
+                    xs_mx(units[m])
             widen(2 * m + 6)
             widen(2 * m + 7)
             if m == 2:
@@ -543,16 +611,15 @@ def tile_multiheadattention_pa_kernel(
             elif m == 3:
                 k_turn(1)
                 k_out(1)
-            elif m > 3:
+            elif m > 3 and m < 17:
                 finish(units[m - 2])
-            if m > 1:
+            if m == 16:
+                xs_rope(unit)
+            elif m > 1:
                 rope(unit, 0)
                 rope(unit, 1)
             group(2 * m + 6, "v")
             quant(2 * m + 4)
             quant(2 * m + 5)
             group(2 * m + 7, "p")
-        for e in range(2):
-            back_turn((7, 1), e)
-            back_out((7, 1), e)
-            back_store((7, 1), slice(e, e + 1))
+        last_finish((7, 1))

@@ -79,15 +79,6 @@ def tile_multiheadattention_pa_kernel(
         bv_m = const.tile([P, 4, 256], F32, name="bv_m")
         biasT = const.tile([P, 20], F32, name="biasT")
 
-        nc.scalar.dma_start(
-            out=wsc[:].rearrange("p (g t) -> p g t", t=4),
-            in_=Wq_scale.rearrange("(g p t) o -> p g (t o)", g=G, p=P, t=4),
-        )
-        for vec, row, n in ((bq, 0, 16), (bk, 16, 2), (bv, 18, 2)):
-            nc.scalar.dma_start(out=brow[row : row + n, :], in_=vec.rearrange("(h d) -> h d", d=P))
-        nc.scalar.dma_start(
-            out=mk_b[:].rearrange("p (j b) -> p j b", b=4), in_=mask[0].rearrange("(j r b) -> r j b", j=2, r=P, b=4)
-        )
         warm = const.tile([P, 1], F32, name="warm")
         nc.scalar.activation(out=warm[:], in_=zero1[:], func=COPY)
 
@@ -123,6 +114,17 @@ def tile_multiheadattention_pa_kernel(
             for a in range(2):
                 traw[(j, a)] = tb_pool.tile([P, 3, 512], BF16, name="traw", tag="traw", align_bytes=256)
                 nc.sync.dma_start(out=traw[(j, a)][:], in_=tab_v[a][j])
+
+        def load_small():
+            nc.sync.dma_start(
+                out=wsc[:].rearrange("p (g t) -> p g t", t=4),
+                in_=Wq_scale.rearrange("(g p t) o -> p g (t o)", g=G, p=P, t=4),
+            )
+            for vec, row, n in ((bq, 0, 16), (bk, 16, 2), (bv, 18, 2)):
+                nc.sync.dma_start(out=brow[row : row + n, :], in_=vec.rearrange("(h d) -> h d", d=P))
+            nc.sync.dma_start(
+                out=mk_b[:].rearrange("p (j b) -> p j b", b=4), in_=mask[0].rearrange("(j r b) -> r j b", j=2, r=P, b=4)
+            )
 
         xt = {}
         xg = {}
@@ -501,6 +503,7 @@ def tile_multiheadattention_pa_kernel(
         load_x(0, 2)
         load_kv(3)
         load_x(0, 3)
+        load_small()
         load_wq(0, 2, 0)
         load_wq(0, 2, 1)
         load_tab(0)
@@ -538,20 +541,20 @@ def tile_multiheadattention_pa_kernel(
         x_quant(0, 2)
         x_turn(0, 3)
         x_out(0, 3, "aa")
-        widen(0)
+        widen(0, 1)
         kv_quant(3)
-        widen(1)
+        widen(1, 1)
         mx_pass((v0, k0), 2)
         x_quant(0, 3)
         group(0, "v")
-        widen(2)
+        tab_gather(0, "v")
+        widen(2, 1)
         group(1, "v")
         quant(0)
-        tab_gather(0, "v")
         quant(1)
         bias_turn()
         mx_pass((v0, k0), 3)
-        widen(3)
+        widen(3, 1)
         rope(v0, 0)
         rope(v0, 1)
         tab_turn(0)

@@ -22,7 +22,7 @@ KP = 8
 VP = 9
 SECTIONS = ((0, 0, 16), (1, 16, 24), (2, 40, 24))
 WBB = {2: 8, 4: 4}
-GRPB = {"v": 3, "p": 1, "a": 2}
+GRPB = {"v": 3, "p": 2, "a": 2}
 
 
 def tile_multiheadattention_pa_kernel(
@@ -69,13 +69,13 @@ def tile_multiheadattention_pa_kernel(
         wsc = const.tile([P, 16], F32, name="wsc")
         mk_b = const.tile([P, 8], BF16, name="mk_b")
         mk = const.tile([P, 8], F32, name="mk")
-        x_codes = const.tile([P, G, 2, 512], U32, name="x_codes", align_bytes=64)
-        x_scales = const.tile([P, G, 2, 512], U8, name="x_scales", align_bytes=64)
-        kv_codes = const.tile([P, G, 512], U32, name="kv_codes", align_bytes=64)
-        kv_scales = const.tile([P, G, 512], U8, name="kv_scales", align_bytes=64)
+        x_codes = const.tile([P, G, 2, 512], U32, name="x_codes", align_bytes=256)
+        x_scales = const.tile([P, G, 2, 512], U8, name="x_scales", align_bytes=256)
+        kv_codes = const.tile([P, G, 512], U32, name="kv_codes", align_bytes=256)
+        kv_scales = const.tile([P, G, 512], U8, name="kv_scales", align_bytes=256)
         tabT = const.tile([P, 2, 1024], BF16, name="tabT")
         bv_b = const.tile([P, 256], BF16, name="bv_b")
-        bq_b = const.tile([P, 256], BF16, name="bq_b")
+        bq_b = {}
         bv_m = const.tile([P, 4, 256], F32, name="bv_m")
         biasT = const.tile([P, 20], F32, name="biasT")
 
@@ -115,11 +115,13 @@ def tile_multiheadattention_pa_kernel(
                 traw[(j, a)] = tb_pool.tile([P, 3, 512], BF16, name="traw", tag="traw", align_bytes=256)
                 nc.sync.dma_start(out=traw[(j, a)][:], in_=tab_v[a][j])
 
-        def load_small():
+        def load_wsc():
             nc.sync.dma_start(
                 out=wsc[:].rearrange("p (g t) -> p g t", t=4),
                 in_=Wq_scale.rearrange("(g p t) o -> p g (t o)", g=G, p=P, t=4),
             )
+
+        def load_small():
             for vec, row, n in ((bq, 0, 16), (bk, 16, 2), (bv, 18, 2)):
                 nc.sync.dma_start(out=brow[row : row + n, :], in_=vec.rearrange("(h d) -> h d", d=P))
             nc.sync.dma_start(
@@ -167,7 +169,7 @@ def tile_multiheadattention_pa_kernel(
                     nc.vector.tensor_scalar(out=out, in0=in_, scalar1=scale, scalar2=None, op0=MULT)
 
         def w_group(hp, g, eng):
-            tag = "grp_" + eng
+            tag = "grp_v" if eng == "v" else "grp_p"
             grp[(hp, g)] = grp_pool.tile([P, 256, 4], BF16, name=tag, tag=tag, bufs=GRPB[eng], align_bytes=64)
             if eng == "v":
                 nc.vector.tensor_copy(
@@ -179,8 +181,8 @@ def tile_multiheadattention_pa_kernel(
 
         def w_quant(hp, g):
             if g == 0:
-                codes = wc_pool.tile([P, G, 256], U32, name="w_codes", tag="w_codes", align_bytes=64)
-                scales = wc_pool.tile([P, G, 256], U8, name="w_scales", tag="w_scales", align_bytes=64)
+                codes = wc_pool.tile([P, G, 256], U32, name="w_codes", tag="w_codes", align_bytes=256)
+                scales = wc_pool.tile([P, G, 256], U8, name="w_scales", tag="w_scales", align_bytes=256)
                 wts[hp] = (codes, scales, 0)
             nc.vector.quantize_mx(
                 out=wts[hp][0][:, g, :].bitcast(FP8X4),
@@ -354,8 +356,9 @@ def tile_multiheadattention_pa_kernel(
                 )
             nc.sync.dma_start(out=out_v[2][j], in_=okv[(VP, j)][:].rearrange("p e b d -> p e (b d)"))
 
-        def load_bq_last(eng):
-            eng.dma_start(out=bq_b[:], in_=bq[14 * P : 16 * P].partition_broadcast(P))
+        def load_bq(hp, eng):
+            bq_b[hp] = const.tile([P, 256], BF16, name="bq_b%d" % hp)
+            eng.dma_start(out=bq_b[hp][:], in_=bq[2 * hp * P : (2 * hp + 2) * P].partition_broadcast(P))
 
         def xs_mx(unit):
             hp, j = unit
@@ -383,7 +386,7 @@ def tile_multiheadattention_pa_kernel(
             for q in range(2):
                 t[q] = uw_pool.tile([P, 2, 256], F32, name="uw0", tag="uw0")
                 nc.vector.tensor_tensor(
-                    out=t[q][:], in0=accs[(unit, q)][:], in1=bq_b[:].unsqueeze(1).to_broadcast([P, 2, 256]), op=ADD
+                    out=t[q][:], in0=accs[(unit, q)][:], in1=bq_b[hp][:].unsqueeze(1).to_broadcast([P, 2, 256]), op=ADD
                 )
             for q in range(2):
                 u[q] = uw_pool.tile([P, 2, 2, P], F32, name="uw0", tag="uw0")
@@ -497,6 +500,7 @@ def tile_multiheadattention_pa_kernel(
 
         load_kv(0)
         load_x(0, 0)
+        load_wsc()
         load_kv(1)
         load_x(0, 1)
         load_kv(2)
@@ -508,7 +512,7 @@ def tile_multiheadattention_pa_kernel(
         load_wq(0, 2, 1)
         load_tab(0)
         load_bv(nc.sync)
-        load_bq_last(nc.sync)
+        load_bq(7, nc.sync)
         load_wq(0, 2, 2)
         load_wq(0, 2, 3)
         load_x(1, 0)
@@ -565,7 +569,7 @@ def tile_multiheadattention_pa_kernel(
         x_out(1, 0, "aa")
         quant(3)
         mx_all((0, 0))
-        widen(4)
+        widen(4, 1)
         rope(k0, 0)
         rope(k0, 1)
         x_turn(1, 1)
@@ -583,17 +587,18 @@ def tile_multiheadattention_pa_kernel(
         finish_kv(0)
         x_quant(1, 3)
         tab_gather(1, "v")
-        widen(5)
-        widen(6)
+        widen(5, 1)
+        widen(6, 1)
         group(4, "v")
         group(5, "p")
-        widen(7)
+        widen(7, 1)
         group(6, "v")
         quant(4)
         quant(5)
         group(7, "p")
 
         units = [v1, k1] + [(hp, j) for hp in range(8) for j in range(2)][1:]
+        XS = ((7, 0),)
         for m, unit in enumerate(units, 1):
             if m == 1:
                 v_mx(1)
@@ -602,21 +607,23 @@ def tile_multiheadattention_pa_kernel(
             elif m == 2:
                 mx_all(k1)
             elif m % 2 == 1:
-                mx_all(unit)
-                if m < 15:
-                    mx_all(units[m])
-                elif m == 15:
-                    xs_mx(units[m])
+                for un in units[m - 1 : m + 1]:
+                    if un in XS:
+                        xs_mx(un)
+                    else:
+                        mx_all(un)
             widen(2 * m + 6)
             widen(2 * m + 7)
+            if m in (8, 10, 12):
+                group(2 * m + 7, "a")
             if m == 2:
                 finish((0, 0))
             elif m == 3:
                 k_turn(1)
                 k_out(1)
-            elif m > 3 and m < 17:
+            elif m > 3 and units[m - 2] not in XS:
                 finish(units[m - 2])
-            if m == 16:
+            if unit in XS:
                 xs_rope(unit)
             elif m > 1:
                 rope(unit, 0)
@@ -624,5 +631,6 @@ def tile_multiheadattention_pa_kernel(
             group(2 * m + 6, "v")
             quant(2 * m + 4)
             quant(2 * m + 5)
-            group(2 * m + 7, "p")
+            if not (m in (8, 10, 12)):
+                group(2 * m + 7, "p")
         last_finish((7, 1))

@@ -22,7 +22,7 @@ KP = 8
 VP = 9
 SECTIONS = ((0, 0, 16), (1, 16, 24), (2, 40, 24))
 WBB = {2: 8, 4: 4}
-GRPB = {"v": 3, "p": 2, "a": 2}
+GRPB = {"v": 3, "p": 2, "a": 2, "b": 3}
 
 
 def tile_multiheadattention_pa_kernel(
@@ -169,7 +169,8 @@ def tile_multiheadattention_pa_kernel(
                     nc.vector.tensor_scalar(out=out, in0=in_, scalar1=scale, scalar2=None, op0=MULT)
 
         def w_group(hp, g, eng):
-            tag = "grp_v" if eng == "v" else "grp_p"
+            tag = "grp_v" if eng in "vb" else "grp_p"
+            eng_is_scalar = eng in "ab"
             grp[(hp, g)] = grp_pool.tile([P, 256, 4], BF16, name=tag, tag=tag, bufs=GRPB[eng], align_bytes=64)
             if eng == "v":
                 nc.vector.tensor_copy(
@@ -177,7 +178,7 @@ def tile_multiheadattention_pa_kernel(
                     in_=wide[(hp, g)][:].rearrange("p t (c i) -> p c t i", i=4),
                 )
             else:
-                copy_on(eng, grp[(hp, g)][:], wide[(hp, g)][:].rearrange("p t n -> p n t"))
+                copy_on("a" if eng_is_scalar else eng, grp[(hp, g)][:], wide[(hp, g)][:].rearrange("p t n -> p n t"))
 
         def w_quant(hp, g):
             if g == 0:
@@ -512,6 +513,7 @@ def tile_multiheadattention_pa_kernel(
         load_wq(0, 2, 1)
         load_tab(0)
         load_bv(nc.sync)
+        load_bq(5, nc.sync)
         load_bq(7, nc.sync)
         load_wq(0, 2, 2)
         load_wq(0, 2, 3)
@@ -598,7 +600,7 @@ def tile_multiheadattention_pa_kernel(
         group(7, "p")
 
         units = [v1, k1] + [(hp, j) for hp in range(8) for j in range(2)][1:]
-        XS = ((7, 0),)
+        XS = ((5, 0), (7, 0),)
         for m, unit in enumerate(units, 1):
             if m == 1:
                 v_mx(1)
@@ -614,7 +616,9 @@ def tile_multiheadattention_pa_kernel(
                         mx_all(un)
             widen(2 * m + 6)
             widen(2 * m + 7)
-            if m in (8, 10, 12):
+            if m in (11, 12,):
+                group(2 * m + 6, "b")
+            if m in (99,):
                 group(2 * m + 7, "a")
             if m == 2:
                 finish((0, 0))
@@ -628,9 +632,10 @@ def tile_multiheadattention_pa_kernel(
             elif m > 1:
                 rope(unit, 0)
                 rope(unit, 1)
-            group(2 * m + 6, "v")
+            if m not in (11, 12,):
+                group(2 * m + 6, "v")
             quant(2 * m + 4)
             quant(2 * m + 5)
-            if not (m in (8, 10, 12)):
+            if not (m in (99,)):
                 group(2 * m + 7, "p")
         last_finish((7, 1))

from contextlib import ExitStack

import concourse.masks as masks
import concourse.mybir as mybir

F32 = mybir.dt.float32
BF16 = mybir.dt.bfloat16
U8 = mybir.dt.uint8
U32 = mybir.dt.uint32
FP8 = mybir.dt.float8_e4m3fn
FP8X4 = mybir.dt.float8_e4m3fn_x4
ADD = mybir.AluOpType.add
MULT = mybir.AluOpType.mult
COPY = mybir.ActivationFunctionType.Copy
IDENT = mybir.ActivationFunctionType.Identity

FLOPS = 2 * 1024 * 2048 * 2560

P = 128
G = 4
KP = 8
VP = 9
SECTIONS = ((0, 0, 16), (1, 16, 24), (2, 40, 24))
WBB = {2: 8, 4: 4}
GRPB = {"v": 3, "p": 2, "a": 2, "b": 3}


def tile_multiheadattention_pa_kernel(
    tc, x, cos, sin, mask, Wq_bytes, Wq_scale, bq, Wk, bk, Wv, bv, out_0, out_1, out_2
):
    nc = tc.nc

    x_v = x[0].rearrange("(j r b) (g k) -> j g r b k", j=2, r=P, b=4, g=G)
    wq_v = Wq_bytes.rearrange("(g p t) n -> g p t n", g=G, p=P, t=4)
    wkv_v = [a.rearrange("(g p t) n -> g p t n", g=G, p=P, t=4) for a in (Wk, Wv)]
    tab_v = [a[:, 0].rearrange("t (j r b) d -> j r t (b d)", j=2, r=P, b=4) for a in (cos, sin)]
    out_v = [a[0].rearrange("h (j r b) d -> j r h (b d)", j=2, r=P, b=4) for a in (out_0, out_1, out_2)]

    with ExitStack() as ctx:
        const = ctx.enter_context(tc.tile_pool(name="const", bufs=1))
        xr_pool = ctx.enter_context(tc.tile_pool(name="xr_pool", bufs=6))
        wb_pool = ctx.enter_context(tc.tile_pool(name="wb_pool", bufs=8))
        kv_pool = ctx.enter_context(tc.tile_pool(name="kv_pool", bufs=4))
        tb_pool = ctx.enter_context(tc.tile_pool(name="tb_pool", bufs=4))
        wc_pool = ctx.enter_context(tc.tile_pool(name="wc_pool", bufs=4))
        xg_pool = ctx.enter_context(tc.tile_pool(name="xg_pool", bufs=2))
        wide_pool = ctx.enter_context(tc.tile_pool(name="wide_pool", bufs=6))
        grp_pool = ctx.enter_context(tc.tile_pool(name="grp_pool", bufs=3))
        uw_pool = ctx.enter_context(tc.tile_pool(name="uw_pool", bufs=6))
        o_pool = ctx.enter_context(tc.tile_pool(name="o_pool", bufs=3))
        acc_pool = ctx.enter_context(tc.psum_pool(name="acc_pool", bufs=4))
        tr_pool = ctx.enter_context(tc.psum_pool(name="tr_pool", bufs=4))
        ctx.enter_context(tc.manual_schedule())

        zero1 = const.tile([P, 1], F32, name="zero1")
        nc.vector.memset(zero1[:], 0.0)
        brow = const.tile([P, P], BF16, name="brow")
        nc.vector.memset(brow[:], 0.0)
        ident_f = const.tile([P, P], F32, name="ident_f")
        masks.make_identity(nc, ident_f[:])
        ident_b = const.tile([P, P], BF16, name="ident_b")
        nc.vector.tensor_copy(out=ident_b[:], in_=ident_f[:])
        swap_f = const.tile([P, P], F32, name="swap_f")
        for half in range(2):
            nc.vector.tensor_copy(
                out=swap_f[:, half * 64 : half * 64 + 64], in_=ident_f[:, 64 - half * 64 : 128 - half * 64]
            )

        wsc = const.tile([P, 16], F32, name="wsc")
        mk_b = const.tile([P, 8], BF16, name="mk_b")
        mk = const.tile([P, 8], F32, name="mk")
        x_codes = const.tile([P, G, 2, 512], U32, name="x_codes", align_bytes=256)
        x_scales = const.tile([P, G, 2, 512], U8, name="x_scales", align_bytes=256)
        kv_codes = const.tile([P, G, 512], U32, name="kv_codes", align_bytes=256)
        kv_scales = const.tile([P, G, 512], U8, name="kv_scales", align_bytes=256)
        tabT = const.tile([P, 2, 1024], BF16, name="tabT")
        bv_b = const.tile([P, 256], BF16, name="bv_b")
        bq_b = {}
        bv_m = const.tile([P, 4, 256], F32, name="bv_m")
        biasT = const.tile([P, 20], F32, name="biasT")

        warm = const.tile([P, 1], F32, name="warm")
        nc.scalar.activation(out=warm[:], in_=zero1[:], func=COPY)

        def copy_on(eng, out, in_):
            if eng == "v":
                nc.vector.tensor_copy(out=out, in_=in_)
            elif eng == "a":
                nc.scalar.copy(out=out, in_=in_)
            else:
                nc.gpsimd.tensor_scalar(out=out, in0=in_, scalar1=1.0, scalar2=0.0, op0=MULT, op1=ADD)

        xr = {}
        wraw = {}
        kvraw = {}
        traw = {}

        def load_x(j, g):
            xr[(j, g)] = xr_pool.tile([P, 4, 512], BF16, name="xr", tag="xr", align_bytes=256)
            nc.sync.dma_start(out=xr[(j, g)][:], in_=x_v[j, g])

        def load_kv(g):
            kvraw[g] = kv_pool.tile([P, 2, 4, 256], BF16, name="kvraw", tag="kvraw", align_bytes=256)
            for m in range(2):
                nc.sync.dma_start(out=kvraw[g][:, m], in_=wkv_v[m][g])

        def load_wq(hp0, n, g):
            wq_sb = wb_pool.tile([P, 4, n * 256], U8, name="wq_sb%d" % n, tag="wq_sb%d" % n, bufs=WBB[n], align_bytes=256)
            nc.sync.dma_start(out=wq_sb[:], in_=wq_v[g][:, :, hp0 * 256 : (hp0 + n) * 256])
            for i in range(n):
                wraw[(hp0 + i, g)] = (wq_sb, i)

        def load_tab(j):
            for a in range(2):
                traw[(j, a)] = tb_pool.tile([P, 3, 512], BF16, name="traw", tag="traw", align_bytes=256)
                nc.sync.dma_start(out=traw[(j, a)][:], in_=tab_v[a][j])

        def load_wsc():
            nc.sync.dma_start(
                out=wsc[:].rearrange("p (g t) -> p g t", t=4),
                in_=Wq_scale.rearrange("(g p t) o -> p g (t o)", g=G, p=P, t=4),
            )

        def load_small():
            for vec, row, n in ((bq, 0, 16), (bk, 16, 2), (bv, 18, 2)):
                nc.sync.dma_start(out=brow[row : row + n, :], in_=vec.rearrange("(h d) -> h d", d=P))
            nc.sync.dma_start(
                out=mk_b[:].rearrange("p (j b) -> p j b", b=4), in_=mask[0].rearrange("(j r b) -> r j b", j=2, r=P, b=4)
            )

        xt = {}
        xg = {}

        def x_turn(j, g):
            for bb in range(2):
                t = tr_pool.tile([P, 2, 2, P], F32, name="xt", tag="tr")
                xt[(j, g, bb)] = t
                for b2 in range(2):
                    words = xr[(j, g)][:, 2 * bb + b2, :].bitcast(F32)
                    for u in range(2):
                        nc.tensor.transpose(out=t[:, b2, u, :], in_=words[:, u::2], identity=ident_f[:])

        def x_out(j, g, eng):
            xg[(j, g)] = xg_pool.tile([P, 4, P, 2], F32, name="xg", tag="xg", align_bytes=64)
            for bb in range(2):
                copy_on(eng[bb], xg[(j, g)][:, 2 * bb : 2 * bb + 2, :, :], xt[(j, g, bb)][:].rearrange("p b u r -> p b r u"))

        def x_quant(j, g):
            nc.vector.quantize_mx(
                out=x_codes[:, g, j, :].bitcast(FP8X4),
                scales=x_scales[:, g, j, :],
                in_=xg[(j, g)][:].rearrange("p b r u -> p (b r u)").bitcast(BF16),
            )

        wide = {}
        grp = {}
        wts = {}

        def w_widen(hp, g, on_vector=0):
            wide[(hp, g)] = wide_pool.tile([P, 4, 256], BF16, name="wide", tag="wide")
            raw, i = wraw[(hp, g)]
            for t in range(4):
                out = wide[(hp, g)][:, t, :]
                in_ = raw[:, t, i * 256 : (i + 1) * 256].bitcast(FP8)
                scale = wsc[:, 4 * g + t : 4 * g + t + 1]
                if t < 4 - on_vector:
                    nc.scalar.activation(out=out, in_=in_, func=COPY, scale=scale)
                else:
                    nc.vector.tensor_scalar(out=out, in0=in_, scalar1=scale, scalar2=None, op0=MULT)

        def w_group(hp, g, eng):
            tag = "grp_v" if eng in "vb" else "grp_p"
            eng_is_scalar = eng in "ab"
            grp[(hp, g)] = grp_pool.tile([P, 256, 4], BF16, name=tag, tag=tag, bufs=GRPB[eng], align_bytes=64)
            if eng == "v":
                nc.vector.tensor_copy(
                    out=grp[(hp, g)][:].rearrange("p (c i) t -> p c t i", i=4),
                    in_=wide[(hp, g)][:].rearrange("p t (c i) -> p c t i", i=4),
                )
            else:
                copy_on("a" if eng_is_scalar else eng, grp[(hp, g)][:], wide[(hp, g)][:].rearrange("p t n -> p n t"))

        def w_quant(hp, g):
            if g == 0:
                codes = wc_pool.tile([P, G, 256], U32, name="w_codes", tag="w_codes", align_bytes=256)
                scales = wc_pool.tile([P, G, 256], U8, name="w_scales", tag="w_scales", align_bytes=256)
                wts[hp] = (codes, scales, 0)
            nc.vector.quantize_mx(
                out=wts[hp][0][:, g, :].bitcast(FP8X4),
                scales=wts[hp][1][:, g, :],
                in_=grp[(hp, g)][:].rearrange("p n t -> p (n t)"),
            )

        wts[KP] = (kv_codes, kv_scales, 0)
        wts[VP] = (kv_codes, kv_scales, 256)

        def kv_group(g, engs):
            grp[(KP, g)] = grp_pool.tile([P, 2, 256, 4], BF16, name="grp_kv", tag="grp_kv", bufs=2, align_bytes=64)
            if len(engs) == 1:
                for m in range(2):
                    nc.vector.tensor_copy(
                        out=grp[(KP, g)][:, m].rearrange("p (c i) t -> p c t i", i=4),
                        in_=kvraw[g][:, m].rearrange("p t (c i) -> p c t i", i=4),
                    )
            else:
                for m in range(2):
                    copy_on(engs[m], grp[(KP, g)][:, m], kvraw[g][:, m].rearrange("p t n -> p n t"))

        def kv_quant(g):
            nc.vector.quantize_mx(
                out=kv_codes[:, g, :].bitcast(FP8X4),
                scales=kv_scales[:, g, :],
                in_=grp[(KP, g)][:].rearrange("p m n t -> p (m n t)"),
            )

        asm = {}

        def tab_gather(j, eng):
            asm[j] = tb_pool.tile([P, 2, 4, P], BF16, name="asm", tag="asm", bufs=2)
            dst = asm[j][:].rearrange("p a b (f i) -> p a b f i", f=2)
            src = [traw[(j, a)][:].rearrange("p t (b f i) -> p t b f i", b=4, f=2) for a in range(2)]
            for tb, c0, n in SECTIONS:
                cs = slice(c0, c0 + n)
                copy_on(eng, dst[:, 0, :, :, cs], src[0][:, tb, :, :, cs])
                copy_on(eng, dst[:, 1, :, 0, cs], src[1][:, tb, :, 1, cs])
                if eng == "a":
                    nc.scalar.activation(out=dst[:, 1, :, 1, cs], in_=src[1][:, tb, :, 0, cs], func=COPY, scale=-1.0)
                elif eng == "v":
                    nc.vector.tensor_scalar(
                        out=dst[:, 1, :, 1, cs], in0=src[1][:, tb, :, 0, cs], scalar1=-1.0, scalar2=None, op0=MULT
                    )
                else:
                    nc.gpsimd.tensor_scalar(
                        out=dst[:, 1, :, 1, cs], in0=src[1][:, tb, :, 0, cs], scalar1=-1.0, scalar2=0.0, op0=MULT, op1=ADD
                    )

        def tab_turn(j):
            pt = tr_pool.tile([P, 2, 4, P], BF16, name="pt", tag="tr")
            for a in range(2):
                for b in range(4):
                    nc.tensor.transpose(out=pt[:, a, b, :], in_=asm[j][:, a, b, :], identity=ident_b[:])
            nc.scalar.copy(out=tabT[:, :, j * 512 : (j + 1) * 512], in_=pt[:].rearrange("p a b r -> p a (b r)"))

        def bias_turn():
            pb = tr_pool.tile([P, P], BF16, name="pb", tag="tr")
            nc.tensor.transpose(out=pb[:], in_=brow[:], identity=ident_b[:])
            nc.vector.tensor_copy(out=biasT[:], in_=pb[:, 0:20])
            nc.vector.tensor_copy(out=mk[:], in_=mk_b[:])

        accs = {}
        uw = {}
        ob = {}
        o_sb = {}

        def mx(unit, e, g):
            hp, j = unit
            if g == 0:
                accs[(unit, e)] = acc_pool.tile([P, 512], F32, name="acc", tag="acc")
            codes, scales, c0 = wts[hp]
            cols = slice(c0 + e * P, c0 + (e + 1) * P)
            nc.tensor.matmul_mx(
                out=accs[(unit, e)][:],
                lhsT=codes[:, g, cols].bitcast(FP8X4),
                lhsT_scale=scales[:, g, cols],
                rhs=x_codes[:, g, j, :].bitcast(FP8X4),
                rhs_scale=x_scales[:, g, j, :],
                start=(g == 0),
                stop=(g == G - 1),
            )

        def rope(unit, e):
            hp, j = unit
            bias = biasT[:, 2 * hp + e : 2 * hp + e + 1]
            acc = accs[(unit, e)]
            if hp == VP:
                uw[(unit, e)] = (uw_pool.tile([P, 512], F32, name="uw0", tag="uw0"),)
                nc.scalar.activation(out=uw[(unit, e)][0][:], in_=acc[:], func=IDENT, bias=bias)
                return
            u = uw_pool.tile([P, 512], F32, name="uw0", tag="uw0")
            w = uw_pool.tile([P, 512], F32, name="uw1", tag="uw1")
            uw[(unit, e)] = (u, w)
            for a in range(2):
                nc.vector.scalar_tensor_tensor(
                    out=uw[(unit, e)][a][:],
                    in0=acc[:],
                    scalar=bias,
                    in1=tabT[:, a, j * 512 : (j + 1) * 512],
                    op0=ADD,
                    op1=MULT,
                )

        def turn_back(dst, unit, e, b):
            parts = uw[(unit, e)]
            bs = slice(b * P, (b + 1) * P)
            if len(parts) == 1:
                nc.tensor.transpose(out=dst, in_=parts[0][:, bs], identity=ident_f[:])
            else:
                nc.tensor.matmul(out=dst, lhsT=parts[0][:, bs], rhs=ident_f[:], is_transpose=True, start=True, stop=False)
                nc.tensor.matmul(out=dst, lhsT=parts[1][:, bs], rhs=swap_f[:], is_transpose=True, start=False, stop=True)


        def back_turn(unit, e):
            ob[(unit, e)] = tr_pool.tile([P, 4, P], F32, name="ob", tag="tr")
            for b in range(4):
                turn_back(ob[(unit, e)][:, b, :], unit, e, b)

        def back_out(unit, e):
            if e == 0:
                o_sb[unit] = o_pool.tile([P, 2, 4, P], F32, name="o", tag="o", align_bytes=256)
            nc.scalar.copy(out=o_sb[unit][:, e], in_=ob[(unit, e)][:])

        def back_store(unit, heads):
            hp, j = unit
            nc.sync.dma_start(
                out=out_v[0][j][:, 2 * hp + heads.start : 2 * hp + heads.stop, :],
                in_=o_sb[unit][:, heads].rearrange("p e b d -> p e (b d)"),
            )

        okv = {}

        def load_bv(eng):
            eng.dma_start(out=bv_b[:], in_=bv.partition_broadcast(P))

        def v_bias(j):
            for b in range(4):
                nc.gpsimd.tensor_scalar(
                    out=bv_m[:, b, :], in0=bv_b[:], scalar1=mk[:, 4 * j + b : 4 * j + b + 1], scalar2=0.0, op0=MULT, op1=ADD
                )

        def v_mx(j):
            for q in range(2):
                acc = acc_pool.tile([P, 2, 256], F32, name="acc", tag="acc")
                accs[("v", j, q)] = acc
                for b2 in range(2):
                    rows = slice((2 * q + b2) * P, (2 * q + b2 + 1) * P)
                    for g in range(G):
                        nc.tensor.matmul_mx(
                            out=acc[:, b2, :],
                            lhsT=x_codes[:, g, j, rows].bitcast(FP8X4),
                            lhsT_scale=x_scales[:, g, j, rows],
                            rhs=kv_codes[:, g, 256:512].bitcast(FP8X4),
                            rhs_scale=kv_scales[:, g, 256:512],
                            start=(g == 0),
                            stop=(g == G - 1),
                        )

        def v_out(j):
            okv[(VP, j)] = o_pool.tile([P, 2, 4, P], F32, name="o", tag="o", align_bytes=256)
            for b in range(4):
                nc.vector.scalar_tensor_tensor(
                    out=okv[(VP, j)][:, :, b, :],
                    in0=accs[("v", j, b // 2)][:, b % 2, :].rearrange("p (e d) -> p e d", e=2),
                    scalar=mk[:, 4 * j + b : 4 * j + b + 1],
                    in1=bv_m[:, b, :].rearrange("p (e d) -> p e d", e=2),
                    op0=MULT,
                    op1=ADD,
                )
            nc.sync.dma_start(out=out_v[2][j], in_=okv[(VP, j)][:].rearrange("p e b d -> p e (b d)"))

        def load_bq(hp, eng):
            bq_b[hp] = const.tile([P, 256], BF16, name="bq_b%d" % hp)
            eng.dma_start(out=bq_b[hp][:], in_=bq[2 * hp * P : (2 * hp + 2) * P].partition_broadcast(P))

        def xs_mx(unit):
            hp, j = unit
            codes, scales, c0 = wts[hp]
            for q in range(2):
                acc = acc_pool.tile([P, 2, 256], F32, name="acc", tag="acc")
                accs[(unit, q)] = acc
                for b2 in range(2):
                    rows = slice((2 * q + b2) * P, (2 * q + b2 + 1) * P)
                    for g in range(G):
                        nc.tensor.matmul_mx(
                            out=acc[:, b2, :],
                            lhsT=x_codes[:, g, j, rows].bitcast(FP8X4),
                            lhsT_scale=x_scales[:, g, j, rows],
                            rhs=codes[:, g, :].bitcast(FP8X4),
                            rhs_scale=scales[:, g, :],
                            start=(g == 0),
                            stop=(g == G - 1),
                        )

        def xs_rope(unit, store=True):
            hp, j = unit
            o_sb[unit] = o_pool.tile([P, 2, 4, P], F32, name="o", tag="o", align_bytes=256)
            t, u, w = {}, {}, {}
            for q in range(2):
                t[q] = uw_pool.tile([P, 2, 256], F32, name="uw0", tag="uw0")
                nc.vector.tensor_tensor(
                    out=t[q][:], in0=accs[(unit, q)][:], in1=bq_b[hp][:].unsqueeze(1).to_broadcast([P, 2, 256]), op=ADD
                )
            for q in range(2):
                u[q] = uw_pool.tile([P, 2, 2, P], F32, name="uw0", tag="uw0")
                w[q] = uw_pool.tile([P, 2, 2, P], F32, name="uw1", tag="uw1")
                for a, dst in ((0, u[q]), (1, w[q])):
                    nc.vector.tensor_tensor(
                        out=dst[:],
                        in0=t[q][:].rearrange("p b (e d) -> p b e d", e=2),
                        in1=asm[j][:, a, 2 * q : 2 * q + 2, :].unsqueeze(2).to_broadcast([P, 2, 2, P]),
                        op=MULT,
                    )
            for q in range(2):
                for half in range(2):
                    lo, hi = 64 * half, 64 - 64 * half
                    nc.vector.tensor_tensor(
                        out=o_sb[unit][:, :, 2 * q : 2 * q + 2, lo : lo + 64],
                        in0=u[q][:, :, :, lo : lo + 64].rearrange("p b e i -> p e b i"),
                        in1=w[q][:, :, :, hi : hi + 64].rearrange("p b e i -> p e b i"),
                        op=ADD,
                    )
            back_store(unit, slice(0, 2))

        def last_finish(unit):
            hp, j = unit
            back_turn(unit, 0)
            back_out(unit, 0)
            back_store(unit, slice(0, 1))
            for bb, copy in ((0, nc.scalar.copy), (1, nc.vector.tensor_copy)):
                t = tr_pool.tile([P, 2, P], F32, name="ob", tag="tr")
                for b2 in range(2):
                    turn_back(t[:, b2, :], unit, 1, 2 * bb + b2)
                copy(out=o_sb[unit][:, 1, 2 * bb : 2 * bb + 2, :], in_=t[:])
                nc.sync.dma_start(
                    out=out_v[0][j][:, 2 * hp + 1, 256 * bb : 256 * (bb + 1)],
                    in_=o_sb[unit][:, 1, 2 * bb : 2 * bb + 2, :].rearrange("p b d -> p (b d)"),
                )

        def k_turn(j):
            for bb in range(2):
                ob[(j, bb)] = tr_pool.tile([P, 2, 2, P], F32, name="obk", tag="tr")
                for b2 in range(2):
                    for e in range(2):
                        turn_back(ob[(j, bb)][:, b2, e, :], (KP, j), e, 2 * bb + b2)

        def k_out(j):
            okv[(KP, j)] = o_pool.tile([P, 2, 4, P], F32, name="o", tag="o", align_bytes=256)
            for b in range(4):
                nc.scalar.activation(
                    out=okv[(KP, j)][:, :, b, :],
                    in_=ob[(j, b // 2)][:, b % 2],
                    func=COPY,
                    scale=mk[:, 4 * j + b : 4 * j + b + 1],
                )
            nc.sync.dma_start(out=out_v[1][j], in_=okv[(KP, j)][:].rearrange("p e b d -> p e (b d)"))

        def kv_turn(j, b):
            ob[(j, b)] = tr_pool.tile([P, 2, 2, P], F32, name="obkv", tag="tr")
            for q in range(2):
                for e in range(2):
                    turn_back(ob[(j, b)][:, q, e, :], (KP + q, j), e, b)

        def kv_out(j, b):
            if b == 0:
                okv[j] = o_pool.tile([P, 2, 2, 4, P], F32, name="okv", tag="okv", bufs=1, align_bytes=256)
            nc.scalar.activation(
                out=okv[j][:, :, :, b, :],
                in_=ob[(j, b)][:],
                func=COPY,
                scale=mk[:, 4 * j + b : 4 * j + b + 1],
            )

        def kv_store(j):
            for q in range(2):
                nc.sync.dma_start(out=out_v[1 + q][j], in_=okv[j][:, q].rearrange("p e b d -> p e (b d)"))

        def mx_pass(pair, g):
            for unit in pair:
                for e in range(2):
                    mx(unit, e, g)

        def mx_all(unit):
            for e in range(2):
                for g in range(G):
                    mx(unit, e, g)

        def finish_kv(j):
            for b in range(4):
                kv_turn(j, b)
                kv_out(j, b)
            kv_store(j)

        def finish(unit):
            for e in range(2):
                back_turn(unit, e)
                back_out(unit, e)
            back_store(unit, slice(0, 2))

        k0, v0, k1, v1 = (KP, 0), (VP, 0), (KP, 1), (VP, 1)

        def widen(s, on_vector=0):
            if s < 32:
                w_widen(s // 4, s % 4, on_vector)

        def group(s, eng):
            if s < 32:
                w_group(s // 4, s % 4, eng)

        def quant(s):
            if s < 32:
                w_quant(s // 4, s % 4)

        load_kv(0)
        load_x(0, 0)
        load_wsc()
        load_kv(1)
        load_x(0, 1)
        load_kv(2)
        load_x(0, 2)
        load_kv(3)
        load_x(0, 3)
        load_small()
        load_wq(0, 2, 0)
        load_wq(0, 2, 1)
        load_tab(0)
        load_bv(nc.sync)
        load_bq(5, nc.sync)
        load_bq(7, nc.sync)
        load_wq(0, 2, 2)
        load_wq(0, 2, 3)
        load_x(1, 0)
        load_x(1, 1)

        kv_group(0, "v")
        x_turn(0, 0)
        load_x(1, 2)
        kv_quant(0)
        x_out(0, 0, "aa")
        kv_group(1, "v")
        x_quant(0, 0)
        x_turn(0, 1)
        load_x(1, 3)
        load_tab(1)
        for g in range(G):
            load_wq(2, 2, g)
        for g in range(G):
            load_wq(4, 4, g)
        kv_quant(1)
        x_out(0, 1, "aa")
        mx_pass((v0, k0), 0)
        kv_group(2, "v")
        x_quant(0, 1)
        x_turn(0, 2)
        x_out(0, 2, "aa")
        mx_pass((v0, k0), 1)
        kv_quant(2)
        kv_group(3, "v")
        x_quant(0, 2)
        x_turn(0, 3)
        x_out(0, 3, "aa")
        widen(0, 1)
        kv_quant(3)
        widen(1, 1)
        mx_pass((v0, k0), 2)
        x_quant(0, 3)
        group(0, "v")
        tab_gather(0, "v")
        widen(2, 1)
        group(1, "v")
        quant(0)
        quant(1)
        bias_turn()
        mx_pass((v0, k0), 3)
        widen(3, 1)
        rope(v0, 0)
        rope(v0, 1)
        tab_turn(0)
        group(2, "v")
        group(3, "v")
        quant(2)
        x_turn(1, 0)
        x_out(1, 0, "aa")
        quant(3)
        mx_all((0, 0))
        widen(4, 1)
        rope(k0, 0)
        rope(k0, 1)
        x_turn(1, 1)
        x_out(1, 1, "aa")
        x_quant(1, 0)
        x_turn(1, 2)
        x_out(1, 2, "aa")
        x_quant(1, 1)
        v_bias(1)
        rope((0, 0), 0)
        rope((0, 0), 1)
        x_turn(1, 3)
        x_out(1, 3, "aa")
        x_quant(1, 2)
        finish_kv(0)
        x_quant(1, 3)
        tab_gather(1, "v")
        widen(5, 1)
        widen(6, 1)
        group(4, "v")
        group(5, "p")
        widen(7, 1)
        group(6, "v")
        quant(4)
        quant(5)
        group(7, "p")

        units = [v1, k1] + [(hp, j) for hp in range(8) for j in range(2)][1:]
        XS = ((5, 0), (7, 0),)
        for m, unit in enumerate(units, 1):
            if m == 1:
                v_mx(1)
                tab_turn(1)
                v_out(1)
            elif m == 2:
                mx_all(k1)
            elif m % 2 == 1:
                for un in units[m - 1 : m + 1]:
                    if un in XS:
                        xs_mx(un)
                    else:
                        mx_all(un)
            widen(2 * m + 6)
            widen(2 * m + 7)
            if m in (11, 12,):
                group(2 * m + 6, "b")
            if m in (99,):
                group(2 * m + 7, "a")
            if m == 2:
                finish((0, 0))
            elif m == 3:
                k_turn(1)
                k_out(1)
            elif m > 3 and units[m - 2] not in XS:
                finish(units[m - 2])
            if unit in XS:
                xs_rope(unit)
            elif m > 1:
                rope(unit, 0)
                rope(unit, 1)
            if m not in (11, 12,):
                group(2 * m + 6, "v")
            quant(2 * m + 4)
            quant(2 * m + 5)
            if not (m in (99,)):
                group(2 * m + 7, "p")
        last_finish((7, 1))
